import numpy as np
import ml_dtypes


def mxq(x, axis, fmt="e4m3"):
    dtype, down = {"e4m3": (ml_dtypes.float8_e4m3fn, 7), "e5m2": (ml_dtypes.float8_e5m2, 14)}[fmt]
    v = np.moveaxis(np.asarray(x, np.float32).astype(ml_dtypes.bfloat16).astype(np.float64), axis, -1)
    blocks = v.reshape(v.shape[:-1] + (-1, 32))
    amax = np.abs(blocks).max(-1, keepdims=True)
    byte = np.maximum(np.where(amax > 0, np.frexp(amax)[1] - 1 + 127, 0) - down, 1)
    scale = np.exp2(byte - 127.0)
    codes = (blocks / scale).astype(np.float32).astype(dtype).astype(np.float64)
    return np.moveaxis((codes * scale).reshape(v.shape), -1, axis)


WIDE = False


def mx_kscale(k):
    if not WIDE:
        return np.ones(k)
    levels = np.array([10, -10, 5, -5, 0])
    a = np.random.permutation(np.resize(levels, k // 512 * 4)).reshape(k // 512, 4)
    idx = np.arange(k)
    return np.exp2(a[idx // 512, idx % 128 // 32])


BF16 = ml_dtypes.bfloat16


def bf(x):
    return np.asarray(x, np.float32).astype(BF16)


def f64(x):
    return np.asarray(x).astype(np.float64)


E2M1 = np.array([0.0, 0.5, 1.0, 1.5, 2.0, 3.0, 4.0, 6.0, -0.0, -0.5, -1.0, -1.5, -2.0, -3.0, -4.0, -6.0])


def pack_weight(w, fmt):
    k, n = w.shape
    w = f64(bf(w)).reshape(k // 32, 32, n)
    amax = np.abs(w).max(1)
    if fmt == "e4m3":
        byte = np.frexp(amax)[1] - 1 + 127 - 7
    else:
        mant, ex = np.frexp(amax / 6.0)
        byte = np.where(mant > 0.5, ex, ex - 1) + 127
    byte = np.clip(np.where(amax > 0, byte, 1), 1, 254)
    scaled = (w * np.exp2(127.0 - byte)[:, None, :]).reshape(k, n).astype(np.float32)
    by_word = np.ascontiguousarray(scaled.reshape(k // 512, 128, 4, n).transpose(0, 1, 3, 2))
    if fmt == "e4m3":
        words = by_word.astype(ml_dtypes.float8_e4m3fn).view(np.uint8)
    else:
        c = by_word.astype(ml_dtypes.float4_e2m1fn).view(np.uint8) & 0xF
        words = c[..., 0::2] | (c[..., 1::2] << 4)
    return np.ascontiguousarray(words), np.ascontiguousarray(byte.astype(np.uint8).reshape(k // 512, 16, n))


def unpack_weight(words, scales, fmt):
    g, p, n, _ = words.shape
    if fmt == "e4m3":
        vals = np.ascontiguousarray(words).view(ml_dtypes.float8_e4m3fn).astype(np.float64)
    else:
        nib = np.empty((g, p, n, 4), np.uint8)
        nib[..., 0::2] = words & 0xF
        nib[..., 1::2] = words >> 4
        vals = E2M1[nib]
    vals = vals * np.repeat(np.exp2(scales.astype(np.float64) - 127.0), 8, axis=1)[..., None]
    return vals.transpose(0, 1, 3, 2).reshape(g * 512, n)

def pack4(w):
    words, scales = pack_weight(w, "e2m1")
    return words.reshape(words.shape[0], 128, -1), scales


def unpack4(words, scales):
    return unpack_weight(words.reshape(words.shape[0], 128, -1, 2), scales, "e2m1")


B, SA, SB, D, H, DH = 4, 768, 256, 512, 4, 128
S = SA + SB
EPS = 1e-6


def make_rope(s, dh):
    pos = np.arange(s, dtype=np.float64)
    inv_freq = 1.0 / (10000.0 ** (np.arange(0, dh, 2, dtype=np.float64) / dh))
    theta = pos[:, None] * inv_freq[None, :]
    cos, sin = np.cos(theta), np.sin(theta)
    row0 = np.stack([cos, -sin], axis=-1)
    row1 = np.stack([sin, cos], axis=-1)
    return np.stack([row0, row1], axis=-2)[None, None]


def rms_norm(x, w):
    return x * (1.0 / np.sqrt(np.mean(x * x, axis=-1, keepdims=True) + EPS)) * w


def apply_rope(x, freqs):
    x_ = x.reshape(*x.shape[:-1], -1, 1, 2)
    out = freqs[..., 0] * x_[..., 0] + freqs[..., 1] * x_[..., 1]
    return out.reshape(x.shape)


def qkv(x, w_kn, b):
    y = (mxq(x, 2, "e4m3") @ w_kn) + b
    y = y.reshape(x.shape[0], x.shape[1], 3 * H, DH).transpose(0, 2, 1, 3)
    return y[:, :H], y[:, H:2 * H], y[:, 2 * H:]


def setup_inputs():
    sa, sb = mx_kscale(D), mx_kscale(D)
    hidden_states_a = bf(np.random.standard_normal((B, SA, D)) * sa)
    hidden_states_b = bf(np.random.standard_normal((B, SB, D)) * sb)
    image_rotary_emb = bf(make_rope(S, DH))
    a_w = np.random.standard_normal((3 * D, D)) / np.sqrt(D) / sa
    a_qkv_b = bf(np.random.standard_normal(3 * D) * 0.2)
    b_w = np.random.standard_normal((3 * D, D)) / np.sqrt(D) / sb
    b_qkv_b = bf(np.random.standard_normal(3 * D) * 0.2)
    a_words, a_scales = pack4(np.ascontiguousarray(a_w.T))
    b_words, b_scales = pack4(np.ascontiguousarray(b_w.T))
    return {
        "hidden_states_a": hidden_states_a,
        "hidden_states_b": hidden_states_b,
        "image_rotary_emb": image_rotary_emb,
        "a_qkv_w_words": a_words,
        "a_qkv_w_scales": a_scales,
        "a_qkv_b": a_qkv_b,
        "b_qkv_w_words": b_words,
        "b_qkv_w_scales": b_scales,
        "b_qkv_b": b_qkv_b,
        "norm_q_a_w": bf(1.5 + 0.15 * np.random.standard_normal(DH)),
        "norm_k_a_w": bf(1.5 + 0.15 * np.random.standard_normal(DH)),
        "norm_q_b_w": bf(1.5 + 0.15 * np.random.standard_normal(DH)),
        "norm_k_b_w": bf(1.5 + 0.15 * np.random.standard_normal(DH)),
    }


def reference(hidden_states_a, hidden_states_b, image_rotary_emb, a_qkv_w_words, a_qkv_w_scales, a_qkv_b,
              b_qkv_w_words, b_qkv_w_scales, b_qkv_b, norm_q_a_w, norm_k_a_w, norm_q_b_w, norm_k_b_w):
    q_a, k_a, v_a = qkv(f64(hidden_states_a), unpack4(a_qkv_w_words, a_qkv_w_scales), f64(a_qkv_b))
    q_a = rms_norm(q_a, f64(norm_q_a_w))
    k_a = rms_norm(k_a, f64(norm_k_a_w))
    q_b, k_b, v_b = qkv(f64(hidden_states_b), unpack4(b_qkv_w_words, b_qkv_w_scales), f64(b_qkv_b))
    q_b = rms_norm(q_b, f64(norm_q_b_w))
    k_b = rms_norm(k_b, f64(norm_k_b_w))
    q = np.concatenate([q_b, q_a], axis=2)
    k = np.concatenate([k_b, k_a], axis=2)
    v = np.concatenate([v_b, v_a], axis=2)
    f = f64(image_rotary_emb)
    return apply_rope(q, f), apply_rope(k, f), v

@@ -1,0 +1,299 @@
+from contextlib import ExitStack
+
+import concourse.mybir as mybir
+from concourse.masks import make_identity
+
+F32 = mybir.dt.float32
+BF16 = mybir.dt.bfloat16
+I32 = mybir.dt.int32
+U32 = mybir.dt.uint32
+U8 = mybir.dt.uint8
+FP8X4 = mybir.dt.float8_e4m3fn_x4
+FP4X4 = mybir.dt.float4_e2m1fn_x4
+ACT = mybir.ActivationFunctionType
+ALU = mybir.AluOpType
+
+P = 128
+BATCH = 4
+HEADS = 4
+MODEL_DIM = 512
+OUT_DIM = 3 * MODEL_DIM
+POSITIONS = 1024
+EPS = 1e-6
+PAIRS = P // 2
+CHUNK_TILES = 4
+CHUNK_TOKENS = CHUNK_TILES * P
+QK_SLOTS = 2 * HEADS
+
+FLOPS = 2 * BATCH * POSITIONS * MODEL_DIM * OUT_DIM
+
+
+def batch_runs(first_tile, tiles_per_batch):
+    runs = []
+    for k in range(CHUNK_TILES):
+        b, j = divmod(first_tile + k, tiles_per_batch)
+        if runs and runs[-1][2] == b:
+            k0, n = runs[-1][0], runs[-1][1]
+            runs[-1] = (k0, n + 1, b, runs[-1][3])
+        else:
+            runs.append((k, 1, b, j))
+    return runs
+
+
+def tile_fluxjointattention_pa_t_kernel(
+    tc,
+    hidden_states_a,
+    hidden_states_b,
+    image_rotary_emb,
+    a_qkv_w_words,
+    a_qkv_w_scales,
+    a_qkv_b,
+    b_qkv_w_words,
+    b_qkv_w_scales,
+    b_qkv_b,
+    norm_q_a_w,
+    norm_k_a_w,
+    norm_q_b_w,
+    norm_k_b_w,
+    out_0,
+    out_1,
+    out_2,
+):
+    nc = tc.nc
+    stream_a = {
+        "name": "a", "index": 0, "x": hidden_states_a, "words": a_qkv_w_words, "scales": a_qkv_w_scales,
+        "bias": a_qkv_b, "gains": (norm_q_a_w, norm_k_a_w), "tiles_per_batch": 6, "first_position": 256,
+    }
+    stream_b = {
+        "name": "b", "index": 1, "x": hidden_states_b, "words": b_qkv_w_words, "scales": b_qkv_w_scales,
+        "bias": b_qkv_b, "gains": (norm_q_b_w, norm_k_b_w), "tiles_per_batch": 2, "first_position": 0,
+    }
+    streams = (stream_a, stream_b)
+    rope_rows = image_rotary_emb.rearrange("a c s m i l -> (a c s) (m i l)")
+
+    with ExitStack() as pools:
+        const = pools.enter_context(tc.tile_pool(name="const", bufs=1))
+        stage = pools.enter_context(tc.tile_pool(name="stage", bufs=2))
+        codes_pool = pools.enter_context(tc.tile_pool(name="codes", bufs=3))
+        feat_pool = pools.enter_context(tc.tile_pool(name="feat", bufs=3))
+        stat_pool = pools.enter_context(tc.tile_pool(name="stat", bufs=4))
+        prod_pool = pools.enter_context(tc.tile_pool(name="prod", bufs=4))
+        out_pool = pools.enter_context(tc.tile_pool(name="out", bufs=2))
+        psum_x = pools.enter_context(tc.psum_pool(name="psum_x", bufs=2))
+        psum_z = pools.enter_context(tc.psum_pool(name="psum_z", bufs=2))
+        psum_y = pools.enter_context(tc.psum_pool(name="psum_y", bufs=3))
+        psum_v = pools.enter_context(tc.psum_pool(name="psum_v", bufs=1))
+
+        def load_tokens(stream, b):
+            j_tiles = stream["tiles_per_batch"]
+            nc.sync.dma_start(
+                out=stream["x_sb"][:, b * j_tiles : (b + 1) * j_tiles, :],
+                in_=stream["x"][b].rearrange("(p j) k -> p j k", j=j_tiles),
+            )
+
+        def load_weights(stream):
+            nc.sync.dma_start(out=stream["words_sb"][:].bitcast(I32), in_=stream["words"][0].bitcast(I32))
+            for quadrant in range(4):
+                nc.sync.dma_start(
+                    out=stream["plane_sb"][32 * quadrant : 32 * quadrant + 4, :].bitcast(I32),
+                    in_=stream["scales"][0, 4 * quadrant : 4 * quadrant + 4, :].bitcast(I32),
+                )
+
+        for stream in streams:
+            x_sb = const.tile([P, BATCH * stream["tiles_per_batch"], MODEL_DIM], BF16, name="x_" + stream["name"])
+            words_sb = const.tile([P, 2 * OUT_DIM], U8, name="words_" + stream["name"], align_bytes=64)
+            plane_sb = const.tile([P, OUT_DIM], U8, name="plane_" + stream["name"], align_bytes=64)
+            rope_sb = const.tile([P, stream["tiles_per_batch"], 2 * P], BF16, name="rope_" + stream["name"])
+            stream["x_sb"] = x_sb
+            stream["words_sb"] = words_sb
+            stream["plane_sb"] = plane_sb
+            stream["rope_sb"] = rope_sb
+            nc.vector.memset(plane_sb[:].bitcast(I32), 0)
+
+        bias_rows = const.tile([P, P], BF16)
+        row_vectors = const.tile([P, 3 * MODEL_DIM], BF16)
+        nc.vector.memset(bias_rows[:], 0.0)
+        nc.vector.memset(row_vectors[:], 0.0)
+
+        load_tokens(stream_a, 0)
+        load_weights(stream_a)
+        for stream in streams:
+            s = stream["index"]
+            nc.scalar.dma_start(
+                out=bias_rows[QK_SLOTS * s : QK_SLOTS * (s + 1), :],
+                in_=stream["bias"].rearrange("(v f) -> v f", f=P)[0:QK_SLOTS, :],
+            )
+            nc.scalar.dma_start(
+                out=row_vectors[0:1, MODEL_DIM * s : MODEL_DIM * (s + 1)],
+                in_=stream["bias"][2 * MODEL_DIM : OUT_DIM].unsqueeze(0),
+            )
+            for qk in range(2):
+                column = 2 * MODEL_DIM + P * (2 * s + qk)
+                nc.scalar.dma_start(out=row_vectors[0:1, column : column + P], in_=stream["gains"][qk].unsqueeze(0))
+            first = stream["first_position"]
+            nc.scalar.dma_start(
+                out=stream["rope_sb"][:],
+                in_=rope_rows[first : first + P * stream["tiles_per_batch"], :].rearrange(
+                    "(p j) e -> p j e", j=stream["tiles_per_batch"]
+                ),
+            )
+        for b in range(1, BATCH):
+            load_tokens(stream_a, b)
+        for b in range(BATCH):
+            load_tokens(stream_b, b)
+        load_weights(stream_b)
+
+        ident = const.tile([P, P], F32)
+        make_identity(nc, ident[:])
+        split_pairs = const.tile([P, P], F32)
+        nc.vector.tensor_copy(
+            out=split_pairs[:].rearrange("p (l m) -> p l m", l=2), in_=ident[:].rearrange("p (m l) -> p l m", l=2)
+        )
+        ones = const.tile([P, P], BF16)
+        nc.vector.memset(ones[:], 1.0)
+        eps = const.tile([P, 1], F32)
+        nc.vector.memset(eps[:], EPS)
+
+        bias_rows_f32 = const.tile([P, P], F32)
+        nc.vector.tensor_copy(out=bias_rows_f32[:], in_=bias_rows[:])
+        bias_ps = psum_x.tile([P, P], F32, tag="x")
+        nc.tensor.transpose(out=bias_ps[:], in_=bias_rows_f32[:], identity=ident[:])
+        bias_columns = const.tile([P, 2 * QK_SLOTS], F32)
+        nc.vector.tensor_copy(out=bias_columns[:], in_=bias_ps[:, 0 : 2 * QK_SLOTS])
+
+        spread = const.tile([P, 3 * MODEL_DIM], F32)
+        for c in range(3):
+            columns = slice(MODEL_DIM * c, MODEL_DIM * (c + 1))
+            spread_ps = psum_x.tile([P, MODEL_DIM], F32, tag="x")
+            nc.tensor.matmul(out=spread_ps[:], lhsT=ones[:], rhs=row_vectors[:, columns], start=True, stop=True)
+            nc.vector.tensor_copy(out=spread[:, columns], in_=spread_ps[:])
+
+        for stream, engine in ((stream_a, nc.vector), (stream_b, nc.gpsimd)):
+            j_tiles = stream["tiles_per_batch"]
+            tables = []
+            for qk in range(2):
+                column = 2 * MODEL_DIM + P * (2 * stream["index"] + qk)
+                gain = spread[:, column : column + P].rearrange("p (m l) -> p l m", l=2)
+                table = const.tile([P, j_tiles, 2, P], F32, name="table_" + stream["name"] + "qk"[qk])
+                for l in range(2):
+                    engine.tensor_tensor(
+                        out=table[:, :, l, :].rearrange("p j (m i) -> p j m i", i=2),
+                        in0=stream["rope_sb"][:].rearrange("p j (m i l) -> p j l m i", i=2, l=2)[:, :, l],
+                        in1=gain[:, l].unsqueeze(1).unsqueeze(3).to_broadcast([P, j_tiles, PAIRS, 2]),
+                        op=ALU.mult,
+                    )
+                tables.append(table)
+            stream["tables"] = tables
+
+        def quantise_chunk(stream, chunk):
+            grouped = stage.tile([P, 4 * CHUNK_TOKENS], BF16, align_bytes=64)
+            grouped_words = grouped[:].bitcast(F32)
+            for half in range(2):
+                xt = psum_x.tile([P, 2, 2, P], F32, tag="x")
+                for tl in range(2):
+                    token_words = stream["x_sb"][:, CHUNK_TILES * chunk + 2 * half + tl, :].bitcast(F32)
+                    for u in range(2):
+                        nc.tensor.transpose(
+                            out=xt[:, tl, u, :], in_=token_words[:, u : MODEL_DIM // 2 : 2], identity=ident[:]
+                        )
+                nc.scalar.copy(
+                    out=grouped_words[:, MODEL_DIM * half : MODEL_DIM * (half + 1)].rearrange(
+                        "p (tl tok u) -> p tl tok u", tl=2, u=2
+                    ),
+                    in_=xt[:].rearrange("p tl u tok -> p tl tok u"),
+                )
+            codes = codes_pool.tile([P, CHUNK_TOKENS], U32, align_bytes=64)
+            code_scales = codes_pool.tile([P, CHUNK_TOKENS], U8, align_bytes=64)
+            nc.vector.quantize_mx(out=codes[:].bitcast(FP8X4), scales=code_scales[:], in_=grouped[:])
+            return codes, code_scales
+
+        def store(out_dram, out_sb, stream, chunk):
+            j_tiles = stream["tiles_per_batch"]
+            first = stream["first_position"]
+            for k0, n, b, j0 in batch_runs(CHUNK_TILES * chunk, j_tiles):
+                nc.sync.dma_start(
+                    out=out_dram[b, :, first : first + P * j_tiles, :].rearrange("h (p j) f -> p h j f", j=j_tiles)[
+                        :, :, j0 : j0 + n, :
+                    ],
+                    in_=out_sb[:, :, k0 : k0 + n, :],
+                )
+
+        def project_values(stream, chunk, codes, code_scales):
+            s = stream["index"]
+            values_bias = spread[:, MODEL_DIM * s : MODEL_DIM * (s + 1)].rearrange("p (h f) -> p h f", h=HEADS)
+            out_v = out_pool.tile([P, HEADS, CHUNK_TILES, P], F32)
+            for k in range(CHUNK_TILES):
+                tokens = slice(P * k, P * (k + 1))
+                zv = psum_v.tile([P, MODEL_DIM], F32)
+                nc.tensor.matmul_mx(
+                    out=zv[:],
+                    lhsT=codes[:, tokens].bitcast(FP8X4),
+                    lhsT_scale=code_scales[:, tokens],
+                    rhs=stream["words_sb"][:, 2 * 2 * MODEL_DIM : 2 * OUT_DIM].bitcast(FP4X4),
+                    rhs_scale=stream["plane_sb"][:, 2 * MODEL_DIM : OUT_DIM],
+                    start=True,
+                    stop=True,
+                )
+                nc.vector.tensor_tensor(
+                    out=out_v[:, :, k, :], in0=zv[:].rearrange("p (h f) -> p h f", h=HEADS), in1=values_bias, op=ALU.add
+                )
+            store(out_2, out_v, stream, chunk)
+
+        def project_and_rotate(stream, chunk, slot, codes, code_scales, out_sb):
+            j_tiles = stream["tiles_per_batch"]
+            table = stream["tables"][slot // HEADS]
+            bias_column = QK_SLOTS * stream["index"] + slot
+            z = psum_z.tile([P, CHUNK_TOKENS], F32)
+            nc.tensor.matmul_mx(
+                out=z[:],
+                lhsT=stream["words_sb"][:, 2 * P * slot : 2 * P * (slot + 1)].bitcast(FP4X4),
+                lhsT_scale=stream["plane_sb"][:, P * slot : P * (slot + 1)],
+                rhs=codes[:].bitcast(FP8X4),
+                rhs_scale=code_scales[:],
+                start=True,
+                stop=True,
+            )
+            y_feat = feat_pool.tile([P, CHUNK_TOKENS], F32)
+            nc.scalar.activation(
+                out=y_feat[:], in_=z[:], func=ACT.Identity, bias=bias_columns[:, bias_column : bias_column + 1], scale=1.0
+            )
+            y = psum_y.tile([P, CHUNK_TILES, P], F32)
+            for k in range(CHUNK_TILES):
+                nc.tensor.transpose(out=y[:, k, :], in_=y_feat[:, P * k : P * (k + 1)], identity=split_pairs[:])
+            squares = stage.tile([P, CHUNK_TILES, P], F32)
+            sum_squares = stat_pool.tile([P, CHUNK_TILES], F32)
+            for k in range(CHUNK_TILES):
+                nc.scalar.activation(
+                    out=squares[:, k, :], in_=y[:, k, :], func=ACT.Square, accum_out=sum_squares[:, k : k + 1]
+                )
+            rms = stat_pool.tile([P, CHUNK_TILES], F32)
+            nc.scalar.activation(out=rms[:], in_=sum_squares[:], func=ACT.Sqrt, bias=eps[:, 0:1], scale=1.0 / P)
+            inv_rms = stat_pool.tile([P, CHUNK_TILES], F32)
+            nc.vector.reciprocal(out=inv_rms[:], in_=rms[:])
+            products = prod_pool.tile([P, CHUNK_TILES, 2, P], F32)
+            for k in range(CHUNK_TILES):
+                j = (CHUNK_TILES * chunk + k) % j_tiles
+                nc.vector.scalar_tensor_tensor(
+                    out=products[:, k].rearrange("p l (m i) -> p (l m) i", i=2),
+                    in0=y[:, k, :].unsqueeze(2).to_broadcast([P, P, 2]),
+                    scalar=inv_rms[:, k : k + 1],
+                    in1=table[:, j].rearrange("p l (m i) -> p (l m) i", i=2),
+                    op0=ALU.mult,
+                    op1=ALU.mult,
+                )
+            nc.gpsimd.tensor_tensor(
+                out=out_sb[:, slot % HEADS], in0=products[:, :, 0, :], in1=products[:, :, 1, :], op=ALU.add
+            )
+
+        work = [(stream, chunk) for stream in streams for chunk in range(BATCH * stream["tiles_per_batch"] // CHUNK_TILES)]
+        quantised = quantise_chunk(work[0][0], work[0][1])
+        for n, (stream, chunk) in enumerate(work):
+            codes, code_scales = quantised
+            if n + 1 < len(work):
+                quantised = quantise_chunk(work[n + 1][0], work[n + 1][1])
+            project_values(stream, chunk, codes, code_scales)
+            for qk, out_dram in enumerate((out_0, out_1)):
+                out_qk = out_pool.tile([P, HEADS, CHUNK_TILES, P], F32, name="out_" + "qk"[qk])
+                for head in range(HEADS):
+                    project_and_rotate(stream, chunk, HEADS * qk + head, codes, code_scales, out_qk)
+                store(out_dram, out_qk, stream, chunk)

@@ -24,6 +24,12 @@ PAIRS = P // 2
 CHUNK_TILES = 4
 CHUNK_TOKENS = CHUNK_TILES * P
 QK_SLOTS = 2 * HEADS
+LAG_BIAS = 1
+LAG_TRANSPOSE = 2
+LAG_NORM = 3
+LAG_PRODUCTS = 4
+LAG_SUM = 5
+PREPARE_TICKS = 6
 
 FLOPS = 2 * BATCH * POSITIONS * MODEL_DIM * OUT_DIM
 
@@ -77,18 +83,20 @@ def tile_fluxjointattention_pa_t_kernel(
         codes_pool = pools.enter_context(tc.tile_pool(name="codes", bufs=3))
         feat_pool = pools.enter_context(tc.tile_pool(name="feat", bufs=3))
         stat_pool = pools.enter_context(tc.tile_pool(name="stat", bufs=4))
-        prod_pool = pools.enter_context(tc.tile_pool(name="prod", bufs=4))
-        out_pool = pools.enter_context(tc.tile_pool(name="out", bufs=2))
-        psum_x = pools.enter_context(tc.psum_pool(name="psum_x", bufs=2))
+        prod_pool = pools.enter_context(tc.tile_pool(name="prod", bufs=3))
+        out_pool = pools.enter_context(tc.tile_pool(name="out", bufs=4))
+        values_pool = pools.enter_context(tc.tile_pool(name="values", bufs=2))
+        psum_x = pools.enter_context(tc.psum_pool(name="psum_x", bufs=1))
         psum_z = pools.enter_context(tc.psum_pool(name="psum_z", bufs=2))
-        psum_y = pools.enter_context(tc.psum_pool(name="psum_y", bufs=3))
+        psum_y = pools.enter_context(tc.psum_pool(name="psum_y", bufs=4))
         psum_v = pools.enter_context(tc.psum_pool(name="psum_v", bufs=1))
 
-        def load_tokens(stream, b):
+        def load_tokens(stream, first_tile, count):
             j_tiles = stream["tiles_per_batch"]
+            b, j0 = divmod(first_tile, j_tiles)
             nc.sync.dma_start(
-                out=stream["x_sb"][:, b * j_tiles : (b + 1) * j_tiles, :],
-                in_=stream["x"][b].rearrange("(p j) k -> p j k", j=j_tiles),
+                out=stream["x_sb"][:, first_tile : first_tile + count, :],
+                in_=stream["x"][b].rearrange("(p j) k -> p j k", j=j_tiles)[:, j0 : j0 + count, :],
             )
 
         def load_weights(stream):
@@ -115,21 +123,24 @@ def tile_fluxjointattention_pa_t_kernel(
         nc.vector.memset(bias_rows[:], 0.0)
         nc.vector.memset(row_vectors[:], 0.0)
 
-        load_tokens(stream_a, 0)
+        load_tokens(stream_a, 0, 2)
         load_weights(stream_a)
+        load_tokens(stream_a, 2, 2)
         for stream in streams:
             s = stream["index"]
             nc.scalar.dma_start(
                 out=bias_rows[QK_SLOTS * s : QK_SLOTS * (s + 1), :],
                 in_=stream["bias"].rearrange("(v f) -> v f", f=P)[0:QK_SLOTS, :],
             )
+        for stream in streams:
+            s = stream["index"]
+            for qk in range(2):
+                column = 2 * MODEL_DIM + P * (2 * s + qk)
+                nc.scalar.dma_start(out=row_vectors[0:1, column : column + P], in_=stream["gains"][qk].unsqueeze(0))
             nc.scalar.dma_start(
                 out=row_vectors[0:1, MODEL_DIM * s : MODEL_DIM * (s + 1)],
                 in_=stream["bias"][2 * MODEL_DIM : OUT_DIM].unsqueeze(0),
             )
-            for qk in range(2):
-                column = 2 * MODEL_DIM + P * (2 * s + qk)
-                nc.scalar.dma_start(out=row_vectors[0:1, column : column + P], in_=stream["gains"][qk].unsqueeze(0))
             first = stream["first_position"]
             nc.scalar.dma_start(
                 out=stream["rope_sb"][:],
@@ -137,10 +148,11 @@ def tile_fluxjointattention_pa_t_kernel(
                     "(p j) e -> p j e", j=stream["tiles_per_batch"]
                 ),
             )
+        load_tokens(stream_a, 4, 2)
         for b in range(1, BATCH):
-            load_tokens(stream_a, b)
+            load_tokens(stream_a, 6 * b, 6)
         for b in range(BATCH):
-            load_tokens(stream_b, b)
+            load_tokens(stream_b, 2 * b, 2)
         load_weights(stream_b)
 
         ident = const.tile([P, P], F32)
@@ -153,18 +165,20 @@ def tile_fluxjointattention_pa_t_kernel(
         nc.vector.memset(ones[:], 1.0)
         eps = const.tile([P, 1], F32)
         nc.vector.memset(eps[:], EPS)
+        first_call = const.tile([P, 1], F32)
+        nc.scalar.activation(out=first_call[:], in_=eps[:], func=ACT.Abs_reciprocal_sqrt)
 
         bias_rows_f32 = const.tile([P, P], F32)
         nc.vector.tensor_copy(out=bias_rows_f32[:], in_=bias_rows[:])
-        bias_ps = psum_x.tile([P, P], F32, tag="x")
+        bias_ps = psum_y.tile([P, P], F32, tag="y")
         nc.tensor.transpose(out=bias_ps[:], in_=bias_rows_f32[:], identity=ident[:])
         bias_columns = const.tile([P, 2 * QK_SLOTS], F32)
         nc.vector.tensor_copy(out=bias_columns[:], in_=bias_ps[:, 0 : 2 * QK_SLOTS])
 
         spread = const.tile([P, 3 * MODEL_DIM], F32)
-        for c in range(3):
+        for c in (2, 0, 1):
             columns = slice(MODEL_DIM * c, MODEL_DIM * (c + 1))
-            spread_ps = psum_x.tile([P, MODEL_DIM], F32, tag="x")
+            spread_ps = psum_y.tile([P, MODEL_DIM], F32, tag="y")
             nc.tensor.matmul(out=spread_ps[:], lhsT=ones[:], rhs=row_vectors[:, columns], start=True, stop=True)
             nc.vector.tensor_copy(out=spread[:, columns], in_=spread_ps[:])
 
@@ -185,64 +199,92 @@ def tile_fluxjointattention_pa_t_kernel(
                 tables.append(table)
             stream["tables"] = tables
 
-        def quantise_chunk(stream, chunk):
-            grouped = stage.tile([P, 4 * CHUNK_TOKENS], BF16, align_bytes=64)
-            grouped_words = grouped[:].bitcast(F32)
-            for half in range(2):
-                xt = psum_x.tile([P, 2, 2, P], F32, tag="x")
-                for tl in range(2):
-                    token_words = stream["x_sb"][:, CHUNK_TILES * chunk + 2 * half + tl, :].bitcast(F32)
-                    for u in range(2):
-                        nc.tensor.transpose(
-                            out=xt[:, tl, u, :], in_=token_words[:, u : MODEL_DIM // 2 : 2], identity=ident[:]
-                        )
-                nc.scalar.copy(
-                    out=grouped_words[:, MODEL_DIM * half : MODEL_DIM * (half + 1)].rearrange(
-                        "p (tl tok u) -> p tl tok u", tl=2, u=2
-                    ),
-                    in_=xt[:].rearrange("p tl u tok -> p tl tok u"),
-                )
+        work = [(stream, chunk) for stream in streams for chunk in range(BATCH * stream["tiles_per_batch"] // CHUNK_TILES)]
+        n_heads = QK_SLOTS * len(work)
+        xt_tiles, grouped_tiles, operands, values_ps, values_sb = {}, {}, {}, {}, {}
+        z_tiles, feat_tiles, y_tiles, sum_tiles, inv_tiles, product_tiles = {}, {}, {}, {}, {}, {}
+
+        def transpose_tokens(w, half):
+            if w >= len(work):
+                return
+            stream, chunk = work[w]
+            xt = psum_x.tile([P, 2, 2, P], F32)
+            for tl in range(2):
+                token_words = stream["x_sb"][:, CHUNK_TILES * chunk + 2 * half + tl, :].bitcast(F32)
+                for u in range(2):
+                    nc.tensor.transpose(out=xt[:, tl, u, :], in_=token_words[:, u : MODEL_DIM // 2 : 2], identity=ident[:])
+            xt_tiles[(w, half)] = xt
+
+        def regroup_tokens(w, half):
+            if w >= len(work):
+                return
+            if half == 0:
+                grouped = stage.tile([P, 4 * CHUNK_TOKENS], BF16, align_bytes=64)
+                grouped_tiles[w] = grouped
+            nc.scalar.copy(
+                out=grouped_tiles[w][:]
+                .bitcast(F32)[:, MODEL_DIM * half : MODEL_DIM * (half + 1)]
+                .rearrange("p (tl tok u) -> p tl tok u", tl=2, u=2),
+                in_=xt_tiles[(w, half)][:].rearrange("p tl u tok -> p tl tok u"),
+            )
+
+        def quantise_tokens(w):
+            if w >= len(work):
+                return
             codes = codes_pool.tile([P, CHUNK_TOKENS], U32, align_bytes=64)
             code_scales = codes_pool.tile([P, CHUNK_TOKENS], U8, align_bytes=64)
-            nc.vector.quantize_mx(out=codes[:].bitcast(FP8X4), scales=code_scales[:], in_=grouped[:])
-            return codes, code_scales
+            nc.vector.quantize_mx(out=codes[:].bitcast(FP8X4), scales=code_scales[:], in_=grouped_tiles[w][:])
+            operands[w] = (codes, code_scales)
 
-        def store(out_dram, out_sb, stream, chunk):
-            j_tiles = stream["tiles_per_batch"]
-            first = stream["first_position"]
-            for k0, n, b, j0 in batch_runs(CHUNK_TILES * chunk, j_tiles):
-                nc.sync.dma_start(
-                    out=out_dram[b, :, first : first + P * j_tiles, :].rearrange("h (p j) f -> p h j f", j=j_tiles)[
-                        :, :, j0 : j0 + n, :
-                    ],
-                    in_=out_sb[:, :, k0 : k0 + n, :],
-                )
+        def multiply_values(w, k):
+            if w < 0 or w >= len(work):
+                return
+            stream = work[w][0]
+            codes, code_scales = operands[w]
+            tokens = slice(P * k, P * (k + 1))
+            zv = psum_v.tile([P, MODEL_DIM], F32)
+            nc.tensor.matmul_mx(
+                out=zv[:],
+                lhsT=codes[:, tokens].bitcast(FP8X4),
+                lhsT_scale=code_scales[:, tokens],
+                rhs=stream["words_sb"][:, 2 * 2 * MODEL_DIM : 2 * OUT_DIM].bitcast(FP4X4),
+                rhs_scale=stream["plane_sb"][:, 2 * MODEL_DIM : OUT_DIM],
+                start=True,
+                stop=True,
+            )
+            values_ps[(w, k)] = zv
 
-        def project_values(stream, chunk, codes, code_scales):
+        def add_values_bias(w, k):
+            if w < 0 or w >= len(work):
+                return
+            stream, chunk = work[w]
             s = stream["index"]
-            values_bias = spread[:, MODEL_DIM * s : MODEL_DIM * (s + 1)].rearrange("p (h f) -> p h f", h=HEADS)
-            out_v = out_pool.tile([P, HEADS, CHUNK_TILES, P], F32)
-            for k in range(CHUNK_TILES):
-                tokens = slice(P * k, P * (k + 1))
-                zv = psum_v.tile([P, MODEL_DIM], F32)
-                nc.tensor.matmul_mx(
-                    out=zv[:],
-                    lhsT=codes[:, tokens].bitcast(FP8X4),
-                    lhsT_scale=code_scales[:, tokens],
-                    rhs=stream["words_sb"][:, 2 * 2 * MODEL_DIM : 2 * OUT_DIM].bitcast(FP4X4),
-                    rhs_scale=stream["plane_sb"][:, 2 * MODEL_DIM : OUT_DIM],
-                    start=True,
-                    stop=True,
-                )
-                nc.vector.tensor_tensor(
-                    out=out_v[:, :, k, :], in0=zv[:].rearrange("p (h f) -> p h f", h=HEADS), in1=values_bias, op=ALU.add
-                )
-            store(out_2, out_v, stream, chunk)
+            if k == 0:
+                out_v = values_pool.tile([P, HEADS, CHUNK_TILES, P], F32)
+                values_sb[w] = out_v
+            nc.vector.tensor_tensor(
+                out=values_sb[w][:, :, k, :],
+                in0=values_ps[(w, k)][:].rearrange("p (h f) -> p h f", h=HEADS),
+                in1=spread[:, MODEL_DIM * s : MODEL_DIM * (s + 1)].rearrange("p (h f) -> p h f", h=HEADS),
+                op=ALU.add,
+            )
+            if k == CHUNK_TILES - 1:
+                j_tiles = stream["tiles_per_batch"]
+                first = stream["first_position"]
+                for k0, n, b, j0 in batch_runs(CHUNK_TILES * chunk, j_tiles):
+                    nc.sync.dma_start(
+                        out=out_2[b, :, first : first + P * j_tiles, :].rearrange("h (p j) f -> p h j f", j=j_tiles)[
+                            :, :, j0 : j0 + n, :
+                        ],
+                        in_=values_sb[w][:, :, k0 : k0 + n, :],
+                    )
 
-        def project_and_rotate(stream, chunk, slot, codes, code_scales, out_sb):
-            j_tiles = stream["tiles_per_batch"]
-            table = stream["tables"][slot // HEADS]
-            bias_column = QK_SLOTS * stream["index"] + slot
+        def multiply(n):
+            if n < 0 or n >= n_heads:
+                return
+            stream = work[n // QK_SLOTS][0]
+            slot = n % QK_SLOTS
+            codes, code_scales = operands[n // QK_SLOTS]
             z = psum_z.tile([P, CHUNK_TOKENS], F32)
             nc.tensor.matmul_mx(
                 out=z[:],
@@ -253,47 +295,106 @@ def tile_fluxjointattention_pa_t_kernel(
                 start=True,
                 stop=True,
             )
+            z_tiles[n] = z
+
+        def add_bias(n):
+            if n < 0 or n >= n_heads:
+                return
+            bias_column = QK_SLOTS * work[n // QK_SLOTS][0]["index"] + n % QK_SLOTS
             y_feat = feat_pool.tile([P, CHUNK_TOKENS], F32)
             nc.scalar.activation(
-                out=y_feat[:], in_=z[:], func=ACT.Identity, bias=bias_columns[:, bias_column : bias_column + 1], scale=1.0
+                out=y_feat[:],
+                in_=z_tiles[n][:],
+                func=ACT.Identity,
+                bias=bias_columns[:, bias_column : bias_column + 1],
+                scale=1.0,
             )
-            y = psum_y.tile([P, CHUNK_TILES, P], F32)
+            feat_tiles[n] = y_feat
+
+        def transpose_back(n):
+            if n < 0 or n >= n_heads:
+                return
+            y = psum_y.tile([P, CHUNK_TILES, P], F32, tag="y")
             for k in range(CHUNK_TILES):
-                nc.tensor.transpose(out=y[:, k, :], in_=y_feat[:, P * k : P * (k + 1)], identity=split_pairs[:])
+                nc.tensor.transpose(out=y[:, k, :], in_=feat_tiles[n][:, P * k : P * (k + 1)], identity=split_pairs[:])
+            y_tiles[n] = y
+
+        def sum_of_squares(n):
+            if n < 0 or n >= n_heads:
+                return
             squares = stage.tile([P, CHUNK_TILES, P], F32)
             sum_squares = stat_pool.tile([P, CHUNK_TILES], F32)
             for k in range(CHUNK_TILES):
                 nc.scalar.activation(
-                    out=squares[:, k, :], in_=y[:, k, :], func=ACT.Square, accum_out=sum_squares[:, k : k + 1]
+                    out=squares[:, k, :], in_=y_tiles[n][:, k, :], func=ACT.Square, accum_out=sum_squares[:, k : k + 1]
                 )
-            rms = stat_pool.tile([P, CHUNK_TILES], F32)
-            nc.scalar.activation(out=rms[:], in_=sum_squares[:], func=ACT.Sqrt, bias=eps[:, 0:1], scale=1.0 / P)
+            sum_tiles[n] = sum_squares
+
+        def inverse_rms(n):
+            if n < 0 or n >= n_heads:
+                return
             inv_rms = stat_pool.tile([P, CHUNK_TILES], F32)
-            nc.vector.reciprocal(out=inv_rms[:], in_=rms[:])
+            nc.scalar.activation(
+                out=inv_rms[:], in_=sum_tiles[n][:], func=ACT.Abs_reciprocal_sqrt, bias=eps[:, 0:1], scale=1.0 / P
+            )
+            inv_tiles[n] = inv_rms
+
+        def rotation_products(n):
+            if n < 0 or n >= n_heads:
+                return
+            stream, chunk = work[n // QK_SLOTS]
+            table = stream["tables"][(n % QK_SLOTS) // HEADS]
             products = prod_pool.tile([P, CHUNK_TILES, 2, P], F32)
             for k in range(CHUNK_TILES):
-                j = (CHUNK_TILES * chunk + k) % j_tiles
+                j = (CHUNK_TILES * chunk + k) % stream["tiles_per_batch"]
                 nc.vector.scalar_tensor_tensor(
                     out=products[:, k].rearrange("p l (m i) -> p (l m) i", i=2),
-                    in0=y[:, k, :].unsqueeze(2).to_broadcast([P, P, 2]),
-                    scalar=inv_rms[:, k : k + 1],
+                    in0=y_tiles[n][:, k, :].unsqueeze(2).to_broadcast([P, P, 2]),
+                    scalar=inv_tiles[n][:, k : k + 1],
                     in1=table[:, j].rearrange("p l (m i) -> p (l m) i", i=2),
                     op0=ALU.mult,
                     op1=ALU.mult,
                 )
-            nc.gpsimd.tensor_tensor(
-                out=out_sb[:, slot % HEADS], in0=products[:, :, 0, :], in1=products[:, :, 1, :], op=ALU.add
-            )
+            product_tiles[n] = products
 
-        work = [(stream, chunk) for stream in streams for chunk in range(BATCH * stream["tiles_per_batch"] // CHUNK_TILES)]
-        quantised = quantise_chunk(work[0][0], work[0][1])
-        for n, (stream, chunk) in enumerate(work):
-            codes, code_scales = quantised
-            if n + 1 < len(work):
-                quantised = quantise_chunk(work[n + 1][0], work[n + 1][1])
-            project_values(stream, chunk, codes, code_scales)
-            for qk, out_dram in enumerate((out_0, out_1)):
-                out_qk = out_pool.tile([P, HEADS, CHUNK_TILES, P], F32, name="out_" + "qk"[qk])
-                for head in range(HEADS):
-                    project_and_rotate(stream, chunk, HEADS * qk + head, codes, code_scales, out_qk)
-                store(out_dram, out_qk, stream, chunk)
+        def rotation_sum(n):
+            if n < 0 or n >= n_heads:
+                return
+            stream, chunk = work[n // QK_SLOTS]
+            out_dram = (out_0, out_1)[(n % QK_SLOTS) // HEADS]
+            head = n % HEADS
+            rotated = out_pool.tile([P, CHUNK_TILES, P], F32)
+            nc.gpsimd.tensor_tensor(
+                out=rotated[:], in0=product_tiles[n][:, :, 0, :], in1=product_tiles[n][:, :, 1, :], op=ALU.add
+            )
+            j_tiles = stream["tiles_per_batch"]
+            first = stream["first_position"]
+            for k0, count, b, j0 in batch_runs(CHUNK_TILES * chunk, j_tiles):
+                nc.sync.dma_start(
+                    out=out_dram[b, head, first : first + P * j_tiles, :].rearrange("(p j) f -> p j f", j=j_tiles)[
+                        :, j0 : j0 + count, :
+                    ],
+                    in_=rotated[:, k0 : k0 + count, :],
+                )
+
+        with tc.manual_schedule():
+            for tick in range(-PREPARE_TICKS, n_heads + LAG_SUM):
+                ahead, phase = divmod(tick + PREPARE_TICKS, QK_SLOTS)
+                now, step = divmod(tick, QK_SLOTS)
+                transpose_back(tick - LAG_TRANSPOSE)
+                if phase in (0, 2):
+                    transpose_tokens(ahead, phase // 2)
+                multiply(tick)
+                if step % 2 == 0:
+                    multiply_values(now, step // 2)
+                sum_of_squares(tick - LAG_NORM)
+                add_bias(tick - LAG_BIAS)
+                inverse_rms(tick - LAG_NORM)
+                if phase in (1, 3):
+                    regroup_tokens(ahead, phase // 2)
+                rotation_products(tick - LAG_PRODUCTS)
+                if step % 2 == 1:
+                    add_values_bias(now, step // 2)
+                if phase == 4:
+                    quantise_tokens(ahead)
+                rotation_sum(tick - LAG_SUM)

@@ -30,6 +30,7 @@ LAG_NORM = 3
 LAG_PRODUCTS = 4
 LAG_SUM = 5
 PREPARE_TICKS = 6
+FIRST_LATE_TABLE = 10
 
 FLOPS = 2 * BATCH * POSITIONS * MODEL_DIM * OUT_DIM
 
@@ -91,6 +92,31 @@ def tile_fluxjointattention_pa_t_kernel(
         psum_y = pools.enter_context(tc.psum_pool(name="psum_y", bufs=4))
         psum_v = pools.enter_context(tc.psum_pool(name="psum_v", bufs=1))
 
+        for stream in streams:
+            x_sb = const.tile([P, BATCH * stream["tiles_per_batch"], MODEL_DIM], BF16, name="x_" + stream["name"])
+            words_sb = const.tile([P, 2 * OUT_DIM], U8, name="words_" + stream["name"], align_bytes=64)
+            plane_sb = const.tile([P, OUT_DIM], U8, name="plane_" + stream["name"], align_bytes=64)
+            rope_sb = const.tile([P, stream["tiles_per_batch"], 2 * P], BF16, name="rope_" + stream["name"])
+            stream["x_sb"] = x_sb
+            stream["words_sb"] = words_sb
+            stream["plane_sb"] = plane_sb
+            stream["rope_sb"] = rope_sb
+            tables = []
+            for qk in range(2):
+                table = const.tile([P, stream["tiles_per_batch"], 2, P], F32, name="table_" + stream["name"] + "qk"[qk])
+                tables.append(table)
+            stream["tables"] = tables
+        bias_rows = const.tile([P, P], BF16)
+        bias_rows_f32 = const.tile([P, P], F32)
+        bias_columns = const.tile([P, 2 * QK_SLOTS], F32)
+        row_vectors = const.tile([P, 3 * MODEL_DIM], BF16)
+        spread = const.tile([P, 3 * MODEL_DIM], F32)
+        ident = const.tile([P, P], F32)
+        split_pairs = const.tile([P, P], F32)
+        ones = const.tile([P, P], BF16)
+        eps = const.tile([P, 1], F32)
+        first_call = const.tile([P, 1], F32)
+
         def load_tokens(stream, first_tile, count):
             j_tiles = stream["tiles_per_batch"]
             b, j0 = divmod(first_tile, j_tiles)
@@ -107,97 +133,32 @@ def tile_fluxjointattention_pa_t_kernel(
                     in_=stream["scales"][0, 4 * quadrant : 4 * quadrant + 4, :].bitcast(I32),
                 )
 
-        for stream in streams:
-            x_sb = const.tile([P, BATCH * stream["tiles_per_batch"], MODEL_DIM], BF16, name="x_" + stream["name"])
-            words_sb = const.tile([P, 2 * OUT_DIM], U8, name="words_" + stream["name"], align_bytes=64)
-            plane_sb = const.tile([P, OUT_DIM], U8, name="plane_" + stream["name"], align_bytes=64)
-            rope_sb = const.tile([P, stream["tiles_per_batch"], 2 * P], BF16, name="rope_" + stream["name"])
-            stream["x_sb"] = x_sb
-            stream["words_sb"] = words_sb
-            stream["plane_sb"] = plane_sb
-            stream["rope_sb"] = rope_sb
-            nc.vector.memset(plane_sb[:].bitcast(I32), 0)
-
-        bias_rows = const.tile([P, P], BF16)
-        row_vectors = const.tile([P, 3 * MODEL_DIM], BF16)
-        nc.vector.memset(bias_rows[:], 0.0)
-        nc.vector.memset(row_vectors[:], 0.0)
-
-        load_tokens(stream_a, 0, 2)
-        load_weights(stream_a)
-        load_tokens(stream_a, 2, 2)
-        for stream in streams:
-            s = stream["index"]
-            nc.scalar.dma_start(
-                out=bias_rows[QK_SLOTS * s : QK_SLOTS * (s + 1), :],
-                in_=stream["bias"].rearrange("(v f) -> v f", f=P)[0:QK_SLOTS, :],
-            )
-        for stream in streams:
-            s = stream["index"]
-            for qk in range(2):
-                column = 2 * MODEL_DIM + P * (2 * s + qk)
-                nc.scalar.dma_start(out=row_vectors[0:1, column : column + P], in_=stream["gains"][qk].unsqueeze(0))
-            nc.scalar.dma_start(
-                out=row_vectors[0:1, MODEL_DIM * s : MODEL_DIM * (s + 1)],
-                in_=stream["bias"][2 * MODEL_DIM : OUT_DIM].unsqueeze(0),
-            )
+        def load_rope(stream, queue):
             first = stream["first_position"]
-            nc.scalar.dma_start(
+            queue.dma_start(
                 out=stream["rope_sb"][:],
                 in_=rope_rows[first : first + P * stream["tiles_per_batch"], :].rearrange(
                     "(p j) e -> p j e", j=stream["tiles_per_batch"]
                 ),
             )
-        load_tokens(stream_a, 4, 2)
-        for b in range(1, BATCH):
-            load_tokens(stream_a, 6 * b, 6)
-        for b in range(BATCH):
-            load_tokens(stream_b, 2 * b, 2)
-        load_weights(stream_b)
 
-        ident = const.tile([P, P], F32)
-        make_identity(nc, ident[:])
-        split_pairs = const.tile([P, P], F32)
-        nc.vector.tensor_copy(
-            out=split_pairs[:].rearrange("p (l m) -> p l m", l=2), in_=ident[:].rearrange("p (m l) -> p l m", l=2)
-        )
-        ones = const.tile([P, P], BF16)
-        nc.vector.memset(ones[:], 1.0)
-        eps = const.tile([P, 1], F32)
-        nc.vector.memset(eps[:], EPS)
-        first_call = const.tile([P, 1], F32)
-        nc.scalar.activation(out=first_call[:], in_=eps[:], func=ACT.Abs_reciprocal_sqrt)
-
-        bias_rows_f32 = const.tile([P, P], F32)
-        nc.vector.tensor_copy(out=bias_rows_f32[:], in_=bias_rows[:])
-        bias_ps = psum_y.tile([P, P], F32, tag="y")
-        nc.tensor.transpose(out=bias_ps[:], in_=bias_rows_f32[:], identity=ident[:])
-        bias_columns = const.tile([P, 2 * QK_SLOTS], F32)
-        nc.vector.tensor_copy(out=bias_columns[:], in_=bias_ps[:, 0 : 2 * QK_SLOTS])
-
-        spread = const.tile([P, 3 * MODEL_DIM], F32)
-        for c in (2, 0, 1):
-            columns = slice(MODEL_DIM * c, MODEL_DIM * (c + 1))
+        def spread_rows(c):
             spread_ps = psum_y.tile([P, MODEL_DIM], F32, tag="y")
-            nc.tensor.matmul(out=spread_ps[:], lhsT=ones[:], rhs=row_vectors[:, columns], start=True, stop=True)
-            nc.vector.tensor_copy(out=spread[:, columns], in_=spread_ps[:])
+            nc.tensor.matmul(
+                out=spread_ps[:], lhsT=ones[:], rhs=row_vectors[:, MODEL_DIM * c : MODEL_DIM * (c + 1)], start=True, stop=True
+            )
+            return spread_ps
 
-        for stream, engine in ((stream_a, nc.vector), (stream_b, nc.gpsimd)):
+        def make_table(stream, qk, l, engine, gains):
             j_tiles = stream["tiles_per_batch"]
-            tables = []
-            for qk in range(2):
-                column = 2 * MODEL_DIM + P * (2 * stream["index"] + qk)
-                gain = spread[:, column : column + P].rearrange("p (m l) -> p l m", l=2)
-                table = const.tile([P, j_tiles, 2, P], F32, name="table_" + stream["name"] + "qk"[qk])
-                for l in range(2):
-                    engine.tensor_tensor(
-                        out=table[:, :, l, :].rearrange("p j (m i) -> p j m i", i=2),
-                        in0=stream["rope_sb"][:].rearrange("p j (m i l) -> p j l m i", i=2, l=2)[:, :, l],
-                        in1=gain[:, l].unsqueeze(1).unsqueeze(3).to_broadcast([P, j_tiles, PAIRS, 2]),
-                        op=ALU.mult,
-                    )
-                tables.append(table)
-            stream["tables"] = tables
+            column = P * (2 * stream["index"] + qk)
+            gain = gains[:, column : column + P].rearrange("p (m l) -> p l m", l=2)
+            engine.tensor_tensor(
+                out=stream["tables"][qk][:, :, l, :].rearrange("p j (m i) -> p j m i", i=2),
+                in0=stream["rope_sb"][:].rearrange("p j (m i l) -> p j l m i", i=2, l=2)[:, :, l],
+                in1=gain[:, l].unsqueeze(1).unsqueeze(3).to_broadcast([P, j_tiles, PAIRS, 2]),
+                op=ALU.mult,
+            )
 
         work = [(stream, chunk) for stream in streams for chunk in range(BATCH * stream["tiles_per_batch"] // CHUNK_TILES)]
         n_heads = QK_SLOTS * len(work)
@@ -208,7 +169,10 @@ def tile_fluxjointattention_pa_t_kernel(
             if w >= len(work):
                 return
             stream, chunk = work[w]
-            xt = psum_x.tile([P, 2, 2, P], F32)
+            if w == 0 and half == 1:
+                xt = psum_z.tile([P, 2, 2, P], F32, tag="z")
+            else:
+                xt = psum_x.tile([P, 2, 2, P], F32, tag="x")
             for tl in range(2):
                 token_words = stream["x_sb"][:, CHUNK_TILES * chunk + 2 * half + tl, :].bitcast(F32)
                 for u in range(2):
@@ -242,7 +206,10 @@ def tile_fluxjointattention_pa_t_kernel(
             stream = work[w][0]
             codes, code_scales = operands[w]
             tokens = slice(P * k, P * (k + 1))
-            zv = psum_v.tile([P, MODEL_DIM], F32)
+            if w == len(work) - 1 and k % 2 == 1:
+                zv = psum_x.tile([P, MODEL_DIM], F32, tag="x")
+            else:
+                zv = psum_v.tile([P, MODEL_DIM], F32, tag="v")
             nc.tensor.matmul_mx(
                 out=zv[:],
                 lhsT=codes[:, tokens].bitcast(FP8X4),
@@ -268,10 +235,10 @@ def tile_fluxjointattention_pa_t_kernel(
                 in1=spread[:, MODEL_DIM * s : MODEL_DIM * (s + 1)].rearrange("p (h f) -> p h f", h=HEADS),
                 op=ALU.add,
             )
-            if k == CHUNK_TILES - 1:
-                j_tiles = stream["tiles_per_batch"]
-                first = stream["first_position"]
-                for k0, n, b, j0 in batch_runs(CHUNK_TILES * chunk, j_tiles):
+            j_tiles = stream["tiles_per_batch"]
+            first = stream["first_position"]
+            for k0, n, b, j0 in batch_runs(CHUNK_TILES * chunk, j_tiles):
+                if k0 + n - 1 == k:
                     nc.sync.dma_start(
                         out=out_2[b, :, first : first + P * j_tiles, :].rearrange("h (p j) f -> p h j f", j=j_tiles)[
                             :, :, j0 : j0 + n, :
@@ -285,7 +252,7 @@ def tile_fluxjointattention_pa_t_kernel(
             stream = work[n // QK_SLOTS][0]
             slot = n % QK_SLOTS
             codes, code_scales = operands[n // QK_SLOTS]
-            z = psum_z.tile([P, CHUNK_TOKENS], F32)
+            z = psum_z.tile([P, CHUNK_TOKENS], F32, tag="z")
             nc.tensor.matmul_mx(
                 out=z[:],
                 lhsT=stream["words_sb"][:, 2 * P * slot : 2 * P * (slot + 1)].bitcast(FP4X4),
@@ -377,24 +344,101 @@ def tile_fluxjointattention_pa_t_kernel(
                     in_=rotated[:, k0 : k0 + count, :],
                 )
 
+        def values_ticks(w, k):
+            if w == 0:
+                return k, k
+            if w == len(work) - 1:
+                return n_heads + k, n_heads + k + 1
+            return QK_SLOTS * w + 2 * k, QK_SLOTS * w + 2 * k + 1
+
+        multiply_at, add_at = {}, {}
+        for w in range(len(work)):
+            for k in range(CHUNK_TILES):
+                tick_multiply, tick_add = values_ticks(w, k)
+                multiply_at.setdefault(tick_multiply, []).append((w, k))
+                add_at.setdefault(tick_add, []).append((w, k))
+
         with tc.manual_schedule():
-            for tick in range(-PREPARE_TICKS, n_heads + LAG_SUM):
+            nc.vector.memset(row_vectors[:], 0.0)
+            nc.vector.memset(bias_rows[:], 0.0)
+            for stream in streams:
+                nc.vector.memset(stream["plane_sb"][:].bitcast(I32), 0)
+            nc.gpsimd.memset(eps[:], EPS)
+            make_identity(nc, ident[:])
+            nc.gpsimd.memset(ones[:], 1.0)
+
+            nc.scalar.activation(out=first_call[:], in_=eps[:], func=ACT.Abs_reciprocal_sqrt)
+
+            load_tokens(stream_a, 0, 2)
+            load_tokens(stream_a, 2, 2)
+            for stream in streams:
+                for qk in range(2):
+                    column = 2 * MODEL_DIM + P * (2 * stream["index"] + qk)
+                    nc.sync.dma_start(out=row_vectors[0:1, column : column + P], in_=stream["gains"][qk].unsqueeze(0))
+            for stream in streams:
+                s = stream["index"]
+                nc.sync.dma_start(
+                    out=bias_rows[QK_SLOTS * s : QK_SLOTS * (s + 1), :],
+                    in_=stream["bias"].rearrange("(v f) -> v f", f=P)[0:QK_SLOTS, :],
+                )
+            load_rope(stream_a, nc.sync)
+            load_weights(stream_a)
+            for stream in streams:
+                s = stream["index"]
+                nc.sync.dma_start(
+                    out=row_vectors[0:1, MODEL_DIM * s : MODEL_DIM * (s + 1)],
+                    in_=stream["bias"][2 * MODEL_DIM : OUT_DIM].unsqueeze(0),
+                )
+            load_tokens(stream_a, 4, 2)
+            for b in range(1, BATCH):
+                load_tokens(stream_a, 6 * b, 6)
+            load_rope(stream_b, nc.sync)
+            for b in range(BATCH):
+                load_tokens(stream_b, 2 * b, 2)
+            load_weights(stream_b)
+
+            nc.vector.tensor_copy(
+                out=split_pairs[:].rearrange("p (l m) -> p l m", l=2), in_=ident[:].rearrange("p (m l) -> p l m", l=2)
+            )
+            nc.vector.tensor_copy(out=bias_rows_f32[:], in_=bias_rows[:])
+            transpose_tokens(0, 0)
+            transpose_tokens(0, 1)
+            gains_ps = spread_rows(2)
+            bias_ps = psum_y.tile([P, P], F32, tag="y")
+            nc.tensor.transpose(out=bias_ps[:], in_=bias_rows_f32[:], identity=ident[:])
+            nc.vector.tensor_copy(out=bias_columns[:], in_=bias_ps[:, 0 : 2 * QK_SLOTS])
+            regroup_tokens(0, 0)
+            regroup_tokens(0, 1)
+            nc.scalar.copy(out=spread[:, 2 * MODEL_DIM : 3 * MODEL_DIM], in_=gains_ps[:])
+            for l in range(2):
+                make_table(stream_a, 0, l, nc.vector, gains_ps)
+            for l in range(2):
+                make_table(stream_a, 1, l, nc.gpsimd, spread[:, 2 * MODEL_DIM : 3 * MODEL_DIM])
+            quantise_tokens(0)
+            for c in range(2):
+                values_bias_ps = spread_rows(c)
+                nc.scalar.copy(out=spread[:, MODEL_DIM * c : MODEL_DIM * (c + 1)], in_=values_bias_ps[:])
+
+            late_tables = [(qk, l) for qk in range(2) for l in range(2)]
+            for tick in range(0, n_heads + LAG_SUM):
                 ahead, phase = divmod(tick + PREPARE_TICKS, QK_SLOTS)
-                now, step = divmod(tick, QK_SLOTS)
                 transpose_back(tick - LAG_TRANSPOSE)
                 if phase in (0, 2):
                     transpose_tokens(ahead, phase // 2)
                 multiply(tick)
-                if step % 2 == 0:
-                    multiply_values(now, step // 2)
+                for w, k in multiply_at.get(tick, []):
+                    multiply_values(w, k)
                 sum_of_squares(tick - LAG_NORM)
                 add_bias(tick - LAG_BIAS)
                 inverse_rms(tick - LAG_NORM)
                 if phase in (1, 3):
                     regroup_tokens(ahead, phase // 2)
                 rotation_products(tick - LAG_PRODUCTS)
-                if step % 2 == 1:
-                    add_values_bias(now, step // 2)
+                for w, k in add_at.get(tick, []):
+                    add_values_bias(w, k)
                 if phase == 4:
                     quantise_tokens(ahead)
+                if 0 <= tick - FIRST_LATE_TABLE < len(late_tables):
+                    qk, l = late_tables[tick - FIRST_LATE_TABLE]
+                    make_table(stream_b, qk, l, nc.gpsimd, spread[:, 2 * MODEL_DIM : 3 * MODEL_DIM])
                 rotation_sum(tick - LAG_SUM)

@@ -29,8 +29,7 @@ LAG_TRANSPOSE = 2
 LAG_NORM = 3
 LAG_PRODUCTS = 4
 LAG_SUM = 5
-PREPARE_TICKS = 6
-FIRST_LATE_TABLE = 10
+PREPARE_TICKS = 11
 
 FLOPS = 2 * BATCH * POSITIONS * MODEL_DIM * OUT_DIM
 
@@ -142,12 +141,10 @@ def tile_fluxjointattention_pa_t_kernel(
                 ),
             )
 
-        def spread_rows(c):
-            spread_ps = psum_y.tile([P, MODEL_DIM], F32, tag="y")
+        def spread_rows(c, spread_ps):
             nc.tensor.matmul(
                 out=spread_ps[:], lhsT=ones[:], rhs=row_vectors[:, MODEL_DIM * c : MODEL_DIM * (c + 1)], start=True, stop=True
             )
-            return spread_ps
 
         def make_table(stream, qk, l, engine, gains):
             j_tiles = stream["tiles_per_batch"]
@@ -165,40 +162,44 @@ def tile_fluxjointattention_pa_t_kernel(
         xt_tiles, grouped_tiles, operands, values_ps, values_sb = {}, {}, {}, {}, {}
         z_tiles, feat_tiles, y_tiles, sum_tiles, inv_tiles, product_tiles = {}, {}, {}, {}, {}, {}
 
-        def transpose_tokens(w, half):
-            if w >= len(work):
-                return
-            stream, chunk = work[w]
-            if w == 0 and half == 1:
-                xt = psum_z.tile([P, 2, 2, P], F32, tag="z")
-            else:
-                xt = psum_x.tile([P, 2, 2, P], F32, tag="x")
-            for tl in range(2):
-                token_words = stream["x_sb"][:, CHUNK_TILES * chunk + 2 * half + tl, :].bitcast(F32)
-                for u in range(2):
-                    nc.tensor.transpose(out=xt[:, tl, u, :], in_=token_words[:, u : MODEL_DIM // 2 : 2], identity=ident[:])
-            xt_tiles[(w, half)] = xt
+        x_bank = psum_x.tile([P, 2, 2, P], F32)
+        head_bank = {}
 
-        def regroup_tokens(w, half):
-            if w >= len(work):
-                return
-            if half == 0:
+        def transpose_tokens(w, i):
+            stream, chunk = work[w]
+            if w == 0 and i >= 2:
+                if i == 2:
+                    spare = psum_z.tile([P, 2, 2, P], F32, tag="z")
+                    head_bank[0] = spare
+                xt = head_bank[0][:, i % 2]
+            else:
+                xt = x_bank[:, i % 2]
+            token_words = stream["x_sb"][:, CHUNK_TILES * chunk + i, :].bitcast(F32)
+            for u in range(2):
+                nc.tensor.transpose(out=xt[:, u, :], in_=token_words[:, u : MODEL_DIM // 2 : 2], identity=ident[:])
+            xt_tiles[(w, i)] = xt
+
+        def regroup_tokens(w, i):
+            if i == 0:
                 grouped = stage.tile([P, 4 * CHUNK_TOKENS], BF16, align_bytes=64)
                 grouped_tiles[w] = grouped
             nc.scalar.copy(
-                out=grouped_tiles[w][:]
-                .bitcast(F32)[:, MODEL_DIM * half : MODEL_DIM * (half + 1)]
-                .rearrange("p (tl tok u) -> p tl tok u", tl=2, u=2),
-                in_=xt_tiles[(w, half)][:].rearrange("p tl u tok -> p tl tok u"),
+                out=grouped_tiles[w][:].bitcast(F32)[:, 2 * P * i : 2 * P * (i + 1)].rearrange("p (tok u) -> p tok u", u=2),
+                in_=xt_tiles[(w, i)].rearrange("p u tok -> p tok u"),
             )
 
-        def quantise_tokens(w):
-            if w >= len(work):
-                return
-            codes = codes_pool.tile([P, CHUNK_TOKENS], U32, align_bytes=64)
-            code_scales = codes_pool.tile([P, CHUNK_TOKENS], U8, align_bytes=64)
-            nc.vector.quantize_mx(out=codes[:].bitcast(FP8X4), scales=code_scales[:], in_=grouped_tiles[w][:])
-            operands[w] = (codes, code_scales)
+        def quantise_tokens(w, i):
+            if i == 0:
+                codes = codes_pool.tile([P, CHUNK_TOKENS], U32, align_bytes=64)
+                code_scales = codes_pool.tile([P, CHUNK_TOKENS], U8, align_bytes=64)
+                operands[w] = (codes, code_scales)
+            codes, code_scales = operands[w]
+            tokens = slice(P * i, P * (i + 1))
+            nc.vector.quantize_mx(
+                out=codes[:, tokens].bitcast(FP8X4),
+                scales=code_scales[:, tokens],
+                in_=grouped_tiles[w][:, 4 * P * i : 4 * P * (i + 1)],
+            )
 
         def multiply_values(w, k):
             if w < 0 or w >= len(work):
@@ -207,7 +208,7 @@ def tile_fluxjointattention_pa_t_kernel(
             codes, code_scales = operands[w]
             tokens = slice(P * k, P * (k + 1))
             if w == len(work) - 1 and k % 2 == 1:
-                zv = psum_x.tile([P, MODEL_DIM], F32, tag="x")
+                zv = psum_z.tile([P, MODEL_DIM], F32, tag="z")
             else:
                 zv = psum_v.tile([P, MODEL_DIM], F32, tag="v")
             nc.tensor.matmul_mx(
@@ -358,6 +359,25 @@ def tile_fluxjointattention_pa_t_kernel(
                 multiply_at.setdefault(tick_multiply, []).append((w, k))
                 add_at.setdefault(tick_add, []).append((w, k))
 
+        def prepare_ticks(w, i):
+            if w == 1:
+                first = 2 + 2 * (i // 2)
+                return first, first + 1, first + 2
+            first = QK_SLOTS * w - PREPARE_TICKS + 2 * i
+            return first, first + 2, first + 3
+
+        transpose_at, regroup_at, quantise_at = {}, {}, {}
+        last_copy = {}
+        for w in range(1, len(work)):
+            for i in range(CHUNK_TILES):
+                tick_transpose, tick_regroup, tick_quantise = prepare_ticks(w, i)
+                tick_transpose = max(tick_transpose, last_copy.get(i % 2, tick_transpose - 1) + 1)
+                assert tick_transpose < tick_regroup
+                last_copy[i % 2] = tick_regroup
+                transpose_at.setdefault(tick_transpose, []).append((w, i))
+                regroup_at.setdefault(tick_regroup, []).append((w, i))
+                quantise_at.setdefault(tick_quantise, []).append((w, i))
+
         with tc.manual_schedule():
             nc.vector.memset(row_vectors[:], 0.0)
             nc.vector.memset(bias_rows[:], 0.0)
@@ -382,6 +402,7 @@ def tile_fluxjointattention_pa_t_kernel(
                     in_=stream["bias"].rearrange("(v f) -> v f", f=P)[0:QK_SLOTS, :],
                 )
             load_rope(stream_a, nc.sync)
+            load_rope(stream_b, nc.sync)
             load_weights(stream_a)
             for stream in streams:
                 s = stream["index"]
@@ -392,7 +413,6 @@ def tile_fluxjointattention_pa_t_kernel(
             load_tokens(stream_a, 4, 2)
             for b in range(1, BATCH):
                 load_tokens(stream_a, 6 * b, 6)
-            load_rope(stream_b, nc.sync)
             for b in range(BATCH):
                 load_tokens(stream_b, 2 * b, 2)
             load_weights(stream_b)
@@ -401,44 +421,47 @@ def tile_fluxjointattention_pa_t_kernel(
                 out=split_pairs[:].rearrange("p (l m) -> p l m", l=2), in_=ident[:].rearrange("p (m l) -> p l m", l=2)
             )
             nc.vector.tensor_copy(out=bias_rows_f32[:], in_=bias_rows[:])
-            transpose_tokens(0, 0)
-            transpose_tokens(0, 1)
-            gains_ps = spread_rows(2)
+            for i in range(CHUNK_TILES):
+                transpose_tokens(0, i)
             bias_ps = psum_y.tile([P, P], F32, tag="y")
+            values_bias_a_ps = psum_y.tile([P, MODEL_DIM], F32, tag="y")
+            values_bias_b_ps = psum_y.tile([P, MODEL_DIM], F32, tag="y")
+            gains_ps = psum_y.tile([P, MODEL_DIM], F32, tag="y")
+            spread_rows(2, gains_ps)
             nc.tensor.transpose(out=bias_ps[:], in_=bias_rows_f32[:], identity=ident[:])
             nc.vector.tensor_copy(out=bias_columns[:], in_=bias_ps[:, 0 : 2 * QK_SLOTS])
-            regroup_tokens(0, 0)
-            regroup_tokens(0, 1)
+            for i in range(CHUNK_TILES):
+                regroup_tokens(0, i)
             nc.scalar.copy(out=spread[:, 2 * MODEL_DIM : 3 * MODEL_DIM], in_=gains_ps[:])
             for l in range(2):
                 make_table(stream_a, 0, l, nc.vector, gains_ps)
             for l in range(2):
                 make_table(stream_a, 1, l, nc.gpsimd, spread[:, 2 * MODEL_DIM : 3 * MODEL_DIM])
-            quantise_tokens(0)
-            for c in range(2):
-                values_bias_ps = spread_rows(c)
+            for i in range(CHUNK_TILES):
+                quantise_tokens(0, i)
+            for c, values_bias_ps in enumerate((values_bias_a_ps, values_bias_b_ps)):
+                spread_rows(c, values_bias_ps)
                 nc.scalar.copy(out=spread[:, MODEL_DIM * c : MODEL_DIM * (c + 1)], in_=values_bias_ps[:])
 
             late_tables = [(qk, l) for qk in range(2) for l in range(2)]
             for tick in range(0, n_heads + LAG_SUM):
-                ahead, phase = divmod(tick + PREPARE_TICKS, QK_SLOTS)
                 transpose_back(tick - LAG_TRANSPOSE)
-                if phase in (0, 2):
-                    transpose_tokens(ahead, phase // 2)
+                for w, i in transpose_at.get(tick, []):
+                    transpose_tokens(w, i)
                 multiply(tick)
                 for w, k in multiply_at.get(tick, []):
                     multiply_values(w, k)
                 sum_of_squares(tick - LAG_NORM)
                 add_bias(tick - LAG_BIAS)
                 inverse_rms(tick - LAG_NORM)
-                if phase in (1, 3):
-                    regroup_tokens(ahead, phase // 2)
+                for w, i in regroup_at.get(tick, []):
+                    regroup_tokens(w, i)
                 rotation_products(tick - LAG_PRODUCTS)
                 for w, k in add_at.get(tick, []):
                     add_values_bias(w, k)
-                if phase == 4:
-                    quantise_tokens(ahead)
-                if 0 <= tick - FIRST_LATE_TABLE < len(late_tables):
-                    qk, l = late_tables[tick - FIRST_LATE_TABLE]
-                    make_table(stream_b, qk, l, nc.gpsimd, spread[:, 2 * MODEL_DIM : 3 * MODEL_DIM])
+                for w, i in quantise_at.get(tick, []):
+                    quantise_tokens(w, i)
+                if tick < len(late_tables):
+                    qk, l = late_tables[tick]
+                    make_table(stream_b, qk, l, nc.vector, gains_ps)
                 rotation_sum(tick - LAG_SUM)

@@ -30,6 +30,7 @@ LAG_NORM = 3
 LAG_PRODUCTS = 4
 LAG_SUM = 5
 PREPARE_TICKS = 11
+GAINS_TICK = 1
 
 FLOPS = 2 * BATCH * POSITIONS * MODEL_DIM * OUT_DIM
 
@@ -124,8 +125,10 @@ def tile_fluxjointattention_pa_t_kernel(
                 in_=stream["x"][b].rearrange("(p j) k -> p j k", j=j_tiles)[:, j0 : j0 + count, :],
             )
 
-        def load_weights(stream):
+        def load_words(stream):
             nc.sync.dma_start(out=stream["words_sb"][:].bitcast(I32), in_=stream["words"][0].bitcast(I32))
+
+        def load_scales(stream):
             for quadrant in range(4):
                 nc.sync.dma_start(
                     out=stream["plane_sb"][32 * quadrant : 32 * quadrant + 4, :].bitcast(I32),
@@ -379,71 +382,71 @@ def tile_fluxjointattention_pa_t_kernel(
                 quantise_at.setdefault(tick_quantise, []).append((w, i))
 
         with tc.manual_schedule():
-            nc.vector.memset(row_vectors[:], 0.0)
+            nc.vector.memset(stream_a["plane_sb"][:].bitcast(I32), 0)
             nc.vector.memset(bias_rows[:], 0.0)
-            for stream in streams:
-                nc.vector.memset(stream["plane_sb"][:].bitcast(I32), 0)
+            nc.vector.memset(row_vectors[:], 0.0)
+            nc.vector.memset(stream_b["plane_sb"][:].bitcast(I32), 0)
             nc.gpsimd.memset(eps[:], EPS)
             make_identity(nc, ident[:])
             nc.gpsimd.memset(ones[:], 1.0)
 
             nc.scalar.activation(out=first_call[:], in_=eps[:], func=ACT.Abs_reciprocal_sqrt)
 
-            load_tokens(stream_a, 0, 2)
-            load_tokens(stream_a, 2, 2)
-            for stream in streams:
-                for qk in range(2):
-                    column = 2 * MODEL_DIM + P * (2 * stream["index"] + qk)
-                    nc.sync.dma_start(out=row_vectors[0:1, column : column + P], in_=stream["gains"][qk].unsqueeze(0))
-            for stream in streams:
+            def load_bias_rows(stream):
                 s = stream["index"]
                 nc.sync.dma_start(
                     out=bias_rows[QK_SLOTS * s : QK_SLOTS * (s + 1), :],
                     in_=stream["bias"].rearrange("(v f) -> v f", f=P)[0:QK_SLOTS, :],
                 )
-            load_rope(stream_a, nc.sync)
-            load_rope(stream_b, nc.sync)
-            load_weights(stream_a)
-            for stream in streams:
+
+            def load_values_bias(stream):
                 s = stream["index"]
                 nc.sync.dma_start(
                     out=row_vectors[0:1, MODEL_DIM * s : MODEL_DIM * (s + 1)],
                     in_=stream["bias"][2 * MODEL_DIM : OUT_DIM].unsqueeze(0),
                 )
+
+            load_tokens(stream_a, 0, 2)
+            load_tokens(stream_a, 2, 2)
+            load_scales(stream_a)
+            load_words(stream_a)
+            load_bias_rows(stream_a)
+            load_bias_rows(stream_b)
+            load_values_bias(stream_a)
+            for stream in streams:
+                for qk in range(2):
+                    column = 2 * MODEL_DIM + P * (2 * stream["index"] + qk)
+                    nc.sync.dma_start(out=row_vectors[0:1, column : column + P], in_=stream["gains"][qk].unsqueeze(0))
+            load_rope(stream_a, nc.sync)
+            load_values_bias(stream_b)
+            load_rope(stream_b, nc.sync)
             load_tokens(stream_a, 4, 2)
             for b in range(1, BATCH):
                 load_tokens(stream_a, 6 * b, 6)
             for b in range(BATCH):
                 load_tokens(stream_b, 2 * b, 2)
-            load_weights(stream_b)
+            load_words(stream_b)
+            load_scales(stream_b)
 
             nc.vector.tensor_copy(
                 out=split_pairs[:].rearrange("p (l m) -> p l m", l=2), in_=ident[:].rearrange("p (m l) -> p l m", l=2)
             )
-            nc.vector.tensor_copy(out=bias_rows_f32[:], in_=bias_rows[:])
             for i in range(CHUNK_TILES):
                 transpose_tokens(0, i)
+            for i in range(CHUNK_TILES):
+                regroup_tokens(0, i)
+            for i in range(CHUNK_TILES):
+                quantise_tokens(0, i)
             bias_ps = psum_y.tile([P, P], F32, tag="y")
             values_bias_a_ps = psum_y.tile([P, MODEL_DIM], F32, tag="y")
             values_bias_b_ps = psum_y.tile([P, MODEL_DIM], F32, tag="y")
             gains_ps = psum_y.tile([P, MODEL_DIM], F32, tag="y")
-            spread_rows(2, gains_ps)
+            nc.scalar.copy(out=bias_rows_f32[:], in_=bias_rows[:])
             nc.tensor.transpose(out=bias_ps[:], in_=bias_rows_f32[:], identity=ident[:])
-            nc.vector.tensor_copy(out=bias_columns[:], in_=bias_ps[:, 0 : 2 * QK_SLOTS])
-            for i in range(CHUNK_TILES):
-                regroup_tokens(0, i)
-            nc.scalar.copy(out=spread[:, 2 * MODEL_DIM : 3 * MODEL_DIM], in_=gains_ps[:])
-            for l in range(2):
-                make_table(stream_a, 0, l, nc.vector, gains_ps)
-            for l in range(2):
-                make_table(stream_a, 1, l, nc.gpsimd, spread[:, 2 * MODEL_DIM : 3 * MODEL_DIM])
-            for i in range(CHUNK_TILES):
-                quantise_tokens(0, i)
-            for c, values_bias_ps in enumerate((values_bias_a_ps, values_bias_b_ps)):
-                spread_rows(c, values_bias_ps)
-                nc.scalar.copy(out=spread[:, MODEL_DIM * c : MODEL_DIM * (c + 1)], in_=values_bias_ps[:])
+            nc.scalar.copy(out=bias_columns[:], in_=bias_ps[:, 0 : 2 * QK_SLOTS])
+            spread_rows(0, values_bias_a_ps)
+            nc.scalar.copy(out=spread[:, 0:MODEL_DIM], in_=values_bias_a_ps[:])
 
-            late_tables = [(qk, l) for qk in range(2) for l in range(2)]
             for tick in range(0, n_heads + LAG_SUM):
                 transpose_back(tick - LAG_TRANSPOSE)
                 for w, i in transpose_at.get(tick, []):
@@ -451,17 +454,29 @@ def tile_fluxjointattention_pa_t_kernel(
                 multiply(tick)
                 for w, k in multiply_at.get(tick, []):
                     multiply_values(w, k)
+                if tick == GAINS_TICK:
+                    spread_rows(2, gains_ps)
+                if tick == GAINS_TICK + 1:
+                    spread_rows(1, values_bias_b_ps)
                 sum_of_squares(tick - LAG_NORM)
                 add_bias(tick - LAG_BIAS)
                 inverse_rms(tick - LAG_NORM)
                 for w, i in regroup_at.get(tick, []):
                     regroup_tokens(w, i)
+                if tick == GAINS_TICK:
+                    nc.scalar.copy(out=spread[:, 2 * MODEL_DIM : 3 * MODEL_DIM], in_=gains_ps[:])
+                if tick == GAINS_TICK + 1:
+                    nc.scalar.copy(out=spread[:, MODEL_DIM : 2 * MODEL_DIM], in_=values_bias_b_ps[:])
                 rotation_products(tick - LAG_PRODUCTS)
                 for w, k in add_at.get(tick, []):
                     add_values_bias(w, k)
                 for w, i in quantise_at.get(tick, []):
                     quantise_tokens(w, i)
-                if tick < len(late_tables):
-                    qk, l = late_tables[tick]
-                    make_table(stream_b, qk, l, nc.vector, gains_ps)
+                if 0 <= tick - GAINS_TICK < 3:
+                    stream, qk = ((stream_a, 0), (stream_b, 0), (stream_b, 1))[tick - GAINS_TICK]
+                    for l in range(2):
+                        make_table(stream, qk, l, nc.vector, gains_ps)
+                if tick == GAINS_TICK:
+                    for l in range(2):
+                        make_table(stream_a, 1, l, nc.gpsimd, spread[:, 2 * MODEL_DIM : 3 * MODEL_DIM])
                 rotation_sum(tick - LAG_SUM)

@@ -30,6 +30,8 @@ LAG_NORM = 3
 LAG_PRODUCTS = 4
 LAG_SUM = 5
 PREPARE_TICKS = 11
+OUT_GROUP = 4
+KEPT_VALUES = 2
 GAINS_TICK = 1
 
 FLOPS = 2 * BATCH * POSITIONS * MODEL_DIM * OUT_DIM
@@ -85,7 +87,7 @@ def tile_fluxjointattention_pa_t_kernel(
         feat_pool = pools.enter_context(tc.tile_pool(name="feat", bufs=3))
         stat_pool = pools.enter_context(tc.tile_pool(name="stat", bufs=4))
         prod_pool = pools.enter_context(tc.tile_pool(name="prod", bufs=3))
-        out_pool = pools.enter_context(tc.tile_pool(name="out", bufs=4))
+        out_pool = pools.enter_context(tc.tile_pool(name="out", bufs=3))
         values_pool = pools.enter_context(tc.tile_pool(name="values", bufs=2))
         psum_x = pools.enter_context(tc.psum_pool(name="psum_x", bufs=1))
         psum_z = pools.enter_context(tc.psum_pool(name="psum_z", bufs=2))
@@ -163,7 +165,7 @@ def tile_fluxjointattention_pa_t_kernel(
         work = [(stream, chunk) for stream in streams for chunk in range(BATCH * stream["tiles_per_batch"] // CHUNK_TILES)]
         n_heads = QK_SLOTS * len(work)
         xt_tiles, grouped_tiles, operands, values_ps, values_sb = {}, {}, {}, {}, {}
-        z_tiles, feat_tiles, y_tiles, sum_tiles, inv_tiles, product_tiles = {}, {}, {}, {}, {}, {}
+        z_tiles, feat_tiles, y_tiles, sum_tiles, inv_tiles, product_tiles, out_tiles, product_groups = {}, {}, {}, {}, {}, {}, {}, {}
 
         x_bank = psum_x.tile([P, 2, 2, P], F32)
         head_bank = {}
@@ -210,7 +212,7 @@ def tile_fluxjointattention_pa_t_kernel(
             stream = work[w][0]
             codes, code_scales = operands[w]
             tokens = slice(P * k, P * (k + 1))
-            if w == len(work) - 1 and k % 2 == 1:
+            if w == len(work) - 1 and k == CHUNK_TILES - 1:
                 zv = psum_z.tile([P, MODEL_DIM], F32, tag="z")
             else:
                 zv = psum_v.tile([P, MODEL_DIM], F32, tag="v")
@@ -315,7 +317,10 @@ def tile_fluxjointattention_pa_t_kernel(
                 return
             stream, chunk = work[n // QK_SLOTS]
             table = stream["tables"][(n % QK_SLOTS) // HEADS]
-            products = prod_pool.tile([P, CHUNK_TILES, 2, P], F32)
+            if n % OUT_GROUP == 0:
+                products_heads = prod_pool.tile([P, OUT_GROUP, CHUNK_TILES, 2, P], F32)
+                product_groups[n // OUT_GROUP] = products_heads
+            products = product_groups[n // OUT_GROUP][:, n % OUT_GROUP]
             for k in range(CHUNK_TILES):
                 j = (CHUNK_TILES * chunk + k) % stream["tiles_per_batch"]
                 nc.vector.scalar_tensor_tensor(
@@ -334,9 +339,12 @@ def tile_fluxjointattention_pa_t_kernel(
             stream, chunk = work[n // QK_SLOTS]
             out_dram = (out_0, out_1)[(n % QK_SLOTS) // HEADS]
             head = n % HEADS
-            rotated = out_pool.tile([P, CHUNK_TILES, P], F32)
+            if n % OUT_GROUP == 0:
+                rotated_heads = out_pool.tile([P, OUT_GROUP, CHUNK_TILES, P], F32)
+                out_tiles[n // OUT_GROUP] = rotated_heads
+            rotated = out_tiles[n // OUT_GROUP][:, n % OUT_GROUP]
             nc.gpsimd.tensor_tensor(
-                out=rotated[:], in0=product_tiles[n][:, :, 0, :], in1=product_tiles[n][:, :, 1, :], op=ALU.add
+                out=rotated, in0=product_tiles[n][:, :, 0, :], in1=product_tiles[n][:, :, 1, :], op=ALU.add
             )
             j_tiles = stream["tiles_per_batch"]
             first = stream["first_position"]
@@ -351,8 +359,8 @@ def tile_fluxjointattention_pa_t_kernel(
         def values_ticks(w, k):
             if w == 0:
                 return k, k
-            if w == len(work) - 1:
-                return n_heads + k, n_heads + k + 1
+            if w == len(work) - 1 and k >= CHUNK_TILES - KEPT_VALUES:
+                return n_heads + LAG_PRODUCTS - 1 - (CHUNK_TILES - 1 - k), n_heads + LAG_PRODUCTS
             return QK_SLOTS * w + 2 * k, QK_SLOTS * w + 2 * k + 1
 
         multiply_at, add_at = {}, {}

from contextlib import ExitStack

import concourse.mybir as mybir
from concourse.masks import make_identity

F32 = mybir.dt.float32
BF16 = mybir.dt.bfloat16
I32 = mybir.dt.int32
U32 = mybir.dt.uint32
U8 = mybir.dt.uint8
FP8X4 = mybir.dt.float8_e4m3fn_x4
FP4X4 = mybir.dt.float4_e2m1fn_x4
ACT = mybir.ActivationFunctionType
ALU = mybir.AluOpType

P = 128
BATCH = 4
HEADS = 4
MODEL_DIM = 512
OUT_DIM = 3 * MODEL_DIM
POSITIONS = 1024
EPS = 1e-6
PAIRS = P // 2
CHUNK_TILES = 4
CHUNK_TOKENS = CHUNK_TILES * P
QK_SLOTS = 2 * HEADS
LAG_BIAS = 1
LAG_TRANSPOSE = 2
LAG_NORM = 3
LAG_PRODUCTS = 4
LAG_SUM = 5
PREPARE_TICKS = 11
OUT_GROUP = 4
KEPT_VALUES = 2
GAINS_TICK = 1

FLOPS = 2 * BATCH * POSITIONS * MODEL_DIM * OUT_DIM


def batch_runs(first_tile, tiles_per_batch):
    runs = []
    for k in range(CHUNK_TILES):
        b, j = divmod(first_tile + k, tiles_per_batch)
        if runs and runs[-1][2] == b:
            k0, n = runs[-1][0], runs[-1][1]
            runs[-1] = (k0, n + 1, b, runs[-1][3])
        else:
            runs.append((k, 1, b, j))
    return runs


def tile_fluxjointattention_pa_t_kernel(
    tc,
    hidden_states_a,
    hidden_states_b,
    image_rotary_emb,
    a_qkv_w_words,
    a_qkv_w_scales,
    a_qkv_b,
    b_qkv_w_words,
    b_qkv_w_scales,
    b_qkv_b,
    norm_q_a_w,
    norm_k_a_w,
    norm_q_b_w,
    norm_k_b_w,
    out_0,
    out_1,
    out_2,
):
    nc = tc.nc
    stream_a = {
        "name": "a", "index": 0, "x": hidden_states_a, "words": a_qkv_w_words, "scales": a_qkv_w_scales,
        "bias": a_qkv_b, "gains": (norm_q_a_w, norm_k_a_w), "tiles_per_batch": 6, "first_position": 256,
    }
    stream_b = {
        "name": "b", "index": 1, "x": hidden_states_b, "words": b_qkv_w_words, "scales": b_qkv_w_scales,
        "bias": b_qkv_b, "gains": (norm_q_b_w, norm_k_b_w), "tiles_per_batch": 2, "first_position": 0,
    }
    streams = (stream_a, stream_b)
    rope_rows = image_rotary_emb.rearrange("a c s m i l -> (a c s) (m i l)")

    with ExitStack() as pools:
        const = pools.enter_context(tc.tile_pool(name="const", bufs=1))
        stage = pools.enter_context(tc.tile_pool(name="stage", bufs=2))
        codes_pool = pools.enter_context(tc.tile_pool(name="codes", bufs=3))
        feat_pool = pools.enter_context(tc.tile_pool(name="feat", bufs=3))
        stat_pool = pools.enter_context(tc.tile_pool(name="stat", bufs=4))
        prod_pool = pools.enter_context(tc.tile_pool(name="prod", bufs=3))
        out_pool = pools.enter_context(tc.tile_pool(name="out", bufs=3))
        values_pool = pools.enter_context(tc.tile_pool(name="values", bufs=2))
        psum_x = pools.enter_context(tc.psum_pool(name="psum_x", bufs=1))
        psum_z = pools.enter_context(tc.psum_pool(name="psum_z", bufs=2))
        psum_y = pools.enter_context(tc.psum_pool(name="psum_y", bufs=4))
        psum_v = pools.enter_context(tc.psum_pool(name="psum_v", bufs=1))

        for stream in streams:
            x_sb = const.tile([P, BATCH * stream["tiles_per_batch"], MODEL_DIM], BF16, name="x_" + stream["name"])
            words_sb = const.tile([P, 2 * OUT_DIM], U8, name="words_" + stream["name"], align_bytes=64)
            plane_sb = const.tile([P, OUT_DIM], U8, name="plane_" + stream["name"], align_bytes=64)
            rope_sb = const.tile([P, stream["tiles_per_batch"], 2 * P], BF16, name="rope_" + stream["name"])
            stream["x_sb"] = x_sb
            stream["words_sb"] = words_sb
            stream["plane_sb"] = plane_sb
            stream["rope_sb"] = rope_sb
            tables = []
            for qk in range(2):
                table = const.tile([P, stream["tiles_per_batch"], 2, P], F32, name="table_" + stream["name"] + "qk"[qk])
                tables.append(table)
            stream["tables"] = tables
        bias_rows = const.tile([P, P], BF16)
        bias_rows_f32 = const.tile([P, P], F32)
        bias_columns = const.tile([P, 2 * QK_SLOTS], F32)
        row_vectors = const.tile([P, 3 * MODEL_DIM], BF16)
        spread = const.tile([P, 3 * MODEL_DIM], F32)
        ident = const.tile([P, P], F32)
        split_pairs = const.tile([P, P], F32)
        ones = const.tile([P, P], BF16)
        eps = const.tile([P, 1], F32)
        first_call = const.tile([P, 1], F32)

        def load_tokens(stream, first_tile, count):
            j_tiles = stream["tiles_per_batch"]
            b, j0 = divmod(first_tile, j_tiles)
            nc.sync.dma_start(
                out=stream["x_sb"][:, first_tile : first_tile + count, :],
                in_=stream["x"][b].rearrange("(p j) k -> p j k", j=j_tiles)[:, j0 : j0 + count, :],
            )

        def load_words(stream):
            nc.sync.dma_start(out=stream["words_sb"][:].bitcast(I32), in_=stream["words"][0].bitcast(I32))

        def load_scales(stream):
            for quadrant in range(4):
                nc.sync.dma_start(
                    out=stream["plane_sb"][32 * quadrant : 32 * quadrant + 4, :].bitcast(I32),
                    in_=stream["scales"][0, 4 * quadrant : 4 * quadrant + 4, :].bitcast(I32),
                )

        def load_rope(stream, queue):
            first = stream["first_position"]
            queue.dma_start(
                out=stream["rope_sb"][:],
                in_=rope_rows[first : first + P * stream["tiles_per_batch"], :].rearrange(
                    "(p j) e -> p j e", j=stream["tiles_per_batch"]
                ),
            )

        def spread_rows(c, spread_ps):
            nc.tensor.matmul(
                out=spread_ps[:], lhsT=ones[:], rhs=row_vectors[:, MODEL_DIM * c : MODEL_DIM * (c + 1)], start=True, stop=True
            )

        def make_table(stream, qk, l, engine, gains):
            j_tiles = stream["tiles_per_batch"]
            column = P * (2 * stream["index"] + qk)
            gain = gains[:, column : column + P].rearrange("p (m l) -> p l m", l=2)
            engine.tensor_tensor(
                out=stream["tables"][qk][:, :, l, :].rearrange("p j (m i) -> p j m i", i=2),
                in0=stream["rope_sb"][:].rearrange("p j (m i l) -> p j l m i", i=2, l=2)[:, :, l],
                in1=gain[:, l].unsqueeze(1).unsqueeze(3).to_broadcast([P, j_tiles, PAIRS, 2]),
                op=ALU.mult,
            )

        work = [(stream, chunk) for stream in streams for chunk in range(BATCH * stream["tiles_per_batch"] // CHUNK_TILES)]
        n_heads = QK_SLOTS * len(work)
        xt_tiles, grouped_tiles, operands, values_ps, values_sb = {}, {}, {}, {}, {}
        z_tiles, feat_tiles, y_tiles, sum_tiles, inv_tiles, product_tiles, out_tiles, product_groups = {}, {}, {}, {}, {}, {}, {}, {}

        x_bank = psum_x.tile([P, 2, 2, P], F32)
        head_bank = {}

        def transpose_tokens(w, i):
            stream, chunk = work[w]
            if w == 0 and i >= 2:
                if i == 2:
                    spare = psum_z.tile([P, 2, 2, P], F32, tag="z")
                    head_bank[0] = spare
                xt = head_bank[0][:, i % 2]
            else:
                xt = x_bank[:, i % 2]
            token_words = stream["x_sb"][:, CHUNK_TILES * chunk + i, :].bitcast(F32)
            for u in range(2):
                nc.tensor.transpose(out=xt[:, u, :], in_=token_words[:, u : MODEL_DIM // 2 : 2], identity=ident[:])
            xt_tiles[(w, i)] = xt

        def regroup_tokens(w, i):
            if i == 0:
                grouped = stage.tile([P, 4 * CHUNK_TOKENS], BF16, align_bytes=64)
                grouped_tiles[w] = grouped
            nc.scalar.copy(
                out=grouped_tiles[w][:].bitcast(F32)[:, 2 * P * i : 2 * P * (i + 1)].rearrange("p (tok u) -> p tok u", u=2),
                in_=xt_tiles[(w, i)].rearrange("p u tok -> p tok u"),
            )

        def quantise_tokens(w, i):
            if i == 0:
                codes = codes_pool.tile([P, CHUNK_TOKENS], U32, align_bytes=64)
                code_scales = codes_pool.tile([P, CHUNK_TOKENS], U8, align_bytes=64)
                operands[w] = (codes, code_scales)
            codes, code_scales = operands[w]
            tokens = slice(P * i, P * (i + 1))
            nc.vector.quantize_mx(
                out=codes[:, tokens].bitcast(FP8X4),
                scales=code_scales[:, tokens],
                in_=grouped_tiles[w][:, 4 * P * i : 4 * P * (i + 1)],
            )

        def multiply_values(w, k):
            if w < 0 or w >= len(work):
                return
            stream = work[w][0]
            codes, code_scales = operands[w]
            tokens = slice(P * k, P * (k + 1))
            if w == len(work) - 1 and k == CHUNK_TILES - 1:
                zv = psum_z.tile([P, MODEL_DIM], F32, tag="z")
            else:
                zv = psum_v.tile([P, MODEL_DIM], F32, tag="v")
            nc.tensor.matmul_mx(
                out=zv[:],
                lhsT=codes[:, tokens].bitcast(FP8X4),
                lhsT_scale=code_scales[:, tokens],
                rhs=stream["words_sb"][:, 2 * 2 * MODEL_DIM : 2 * OUT_DIM].bitcast(FP4X4),
                rhs_scale=stream["plane_sb"][:, 2 * MODEL_DIM : OUT_DIM],
                start=True,
                stop=True,
            )
            values_ps[(w, k)] = zv

        def add_values_bias(w, k):
            if w < 0 or w >= len(work):
                return
            stream, chunk = work[w]
            s = stream["index"]
            if k == 0:
                out_v = values_pool.tile([P, HEADS, CHUNK_TILES, P], F32)
                values_sb[w] = out_v
            nc.vector.tensor_tensor(
                out=values_sb[w][:, :, k, :],
                in0=values_ps[(w, k)][:].rearrange("p (h f) -> p h f", h=HEADS),
                in1=spread[:, MODEL_DIM * s : MODEL_DIM * (s + 1)].rearrange("p (h f) -> p h f", h=HEADS),
                op=ALU.add,
            )
            j_tiles = stream["tiles_per_batch"]
            first = stream["first_position"]
            for k0, n, b, j0 in batch_runs(CHUNK_TILES * chunk, j_tiles):
                if k0 + n - 1 == k:
                    nc.sync.dma_start(
                        out=out_2[b, :, first : first + P * j_tiles, :].rearrange("h (p j) f -> p h j f", j=j_tiles)[
                            :, :, j0 : j0 + n, :
                        ],
                        in_=values_sb[w][:, :, k0 : k0 + n, :],
                    )

        def multiply(n):
            if n < 0 or n >= n_heads:
                return
            stream = work[n // QK_SLOTS][0]
            slot = n % QK_SLOTS
            codes, code_scales = operands[n // QK_SLOTS]
            z = psum_z.tile([P, CHUNK_TOKENS], F32, tag="z")
            nc.tensor.matmul_mx(
                out=z[:],
                lhsT=stream["words_sb"][:, 2 * P * slot : 2 * P * (slot + 1)].bitcast(FP4X4),
                lhsT_scale=stream["plane_sb"][:, P * slot : P * (slot + 1)],
                rhs=codes[:].bitcast(FP8X4),
                rhs_scale=code_scales[:],
                start=True,
                stop=True,
            )
            z_tiles[n] = z

        def add_bias(n):
            if n < 0 or n >= n_heads:
                return
            bias_column = QK_SLOTS * work[n // QK_SLOTS][0]["index"] + n % QK_SLOTS
            y_feat = feat_pool.tile([P, CHUNK_TOKENS], F32)
            nc.scalar.activation(
                out=y_feat[:],
                in_=z_tiles[n][:],
                func=ACT.Identity,
                bias=bias_columns[:, bias_column : bias_column + 1],
                scale=1.0,
            )
            feat_tiles[n] = y_feat

        def transpose_back(n):
            if n < 0 or n >= n_heads:
                return
            y = psum_y.tile([P, CHUNK_TILES, P], F32, tag="y")
            for k in range(CHUNK_TILES):
                nc.tensor.transpose(out=y[:, k, :], in_=feat_tiles[n][:, P * k : P * (k + 1)], identity=split_pairs[:])
            y_tiles[n] = y

        def sum_of_squares(n):
            if n < 0 or n >= n_heads:
                return
            squares = stage.tile([P, CHUNK_TILES, P], F32)
            sum_squares = stat_pool.tile([P, CHUNK_TILES], F32)
            for k in range(CHUNK_TILES):
                nc.scalar.activation(
                    out=squares[:, k, :], in_=y_tiles[n][:, k, :], func=ACT.Square, accum_out=sum_squares[:, k : k + 1]
                )
            sum_tiles[n] = sum_squares

        def inverse_rms(n):
            if n < 0 or n >= n_heads:
                return
            inv_rms = stat_pool.tile([P, CHUNK_TILES], F32)
            nc.scalar.activation(
                out=inv_rms[:], in_=sum_tiles[n][:], func=ACT.Abs_reciprocal_sqrt, bias=eps[:, 0:1], scale=1.0 / P
            )
            inv_tiles[n] = inv_rms

        def rotation_products(n):
            if n < 0 or n >= n_heads:
                return
            stream, chunk = work[n // QK_SLOTS]
            table = stream["tables"][(n % QK_SLOTS) // HEADS]
            if n % OUT_GROUP == 0:
                products_heads = prod_pool.tile([P, OUT_GROUP, CHUNK_TILES, 2, P], F32)
                product_groups[n // OUT_GROUP] = products_heads
            products = product_groups[n // OUT_GROUP][:, n % OUT_GROUP]
            for k in range(CHUNK_TILES):
                j = (CHUNK_TILES * chunk + k) % stream["tiles_per_batch"]
                nc.vector.scalar_tensor_tensor(
                    out=products[:, k].rearrange("p l (m i) -> p (l m) i", i=2),
                    in0=y_tiles[n][:, k, :].unsqueeze(2).to_broadcast([P, P, 2]),
                    scalar=inv_tiles[n][:, k : k + 1],
                    in1=table[:, j].rearrange("p l (m i) -> p (l m) i", i=2),
                    op0=ALU.mult,
                    op1=ALU.mult,
                )
            product_tiles[n] = products

        def rotation_sum(n):
            if n < 0 or n >= n_heads:
                return
            stream, chunk = work[n // QK_SLOTS]
            out_dram = (out_0, out_1)[(n % QK_SLOTS) // HEADS]
            head = n % HEADS
            if n % OUT_GROUP == 0:
                rotated_heads = out_pool.tile([P, OUT_GROUP, CHUNK_TILES, P], F32)
                out_tiles[n // OUT_GROUP] = rotated_heads
            rotated = out_tiles[n // OUT_GROUP][:, n % OUT_GROUP]
            nc.gpsimd.tensor_tensor(
                out=rotated, in0=product_tiles[n][:, :, 0, :], in1=product_tiles[n][:, :, 1, :], op=ALU.add
            )
            j_tiles = stream["tiles_per_batch"]
            first = stream["first_position"]
            for k0, count, b, j0 in batch_runs(CHUNK_TILES * chunk, j_tiles):
                nc.sync.dma_start(
                    out=out_dram[b, head, first : first + P * j_tiles, :].rearrange("(p j) f -> p j f", j=j_tiles)[
                        :, j0 : j0 + count, :
                    ],
                    in_=rotated[:, k0 : k0 + count, :],
                )

        def values_ticks(w, k):
            if w == 0:
                return k, k
            if w == len(work) - 1 and k >= CHUNK_TILES - KEPT_VALUES:
                return n_heads + LAG_PRODUCTS - 1 - (CHUNK_TILES - 1 - k), n_heads + LAG_PRODUCTS
            return QK_SLOTS * w + 2 * k, QK_SLOTS * w + 2 * k + 1

        multiply_at, add_at = {}, {}
        for w in range(len(work)):
            for k in range(CHUNK_TILES):
                tick_multiply, tick_add = values_ticks(w, k)
                multiply_at.setdefault(tick_multiply, []).append((w, k))
                add_at.setdefault(tick_add, []).append((w, k))

        def prepare_ticks(w, i):
            if w == 1:
                first = 2 + 2 * (i // 2)
                return first, first + 1, first + 2
            first = QK_SLOTS * w - PREPARE_TICKS + 2 * i
            return first, first + 2, first + 3

        transpose_at, regroup_at, quantise_at = {}, {}, {}
        last_copy = {}
        for w in range(1, len(work)):
            for i in range(CHUNK_TILES):
                tick_transpose, tick_regroup, tick_quantise = prepare_ticks(w, i)
                tick_transpose = max(tick_transpose, last_copy.get(i % 2, tick_transpose - 1) + 1)
                assert tick_transpose < tick_regroup
                last_copy[i % 2] = tick_regroup
                transpose_at.setdefault(tick_transpose, []).append((w, i))
                regroup_at.setdefault(tick_regroup, []).append((w, i))
                quantise_at.setdefault(tick_quantise, []).append((w, i))

        with tc.manual_schedule():
            nc.vector.memset(stream_a["plane_sb"][:].bitcast(I32), 0)
            nc.vector.memset(bias_rows[:], 0.0)
            nc.vector.memset(row_vectors[:], 0.0)
            nc.vector.memset(stream_b["plane_sb"][:].bitcast(I32), 0)
            nc.gpsimd.memset(eps[:], EPS)
            make_identity(nc, ident[:])
            nc.gpsimd.memset(ones[:], 1.0)

            nc.scalar.activation(out=first_call[:], in_=eps[:], func=ACT.Abs_reciprocal_sqrt)

            def load_bias_rows(stream):
                s = stream["index"]
                nc.sync.dma_start(
                    out=bias_rows[QK_SLOTS * s : QK_SLOTS * (s + 1), :],
                    in_=stream["bias"].rearrange("(v f) -> v f", f=P)[0:QK_SLOTS, :],
                )

            def load_values_bias(stream):
                s = stream["index"]
                nc.sync.dma_start(
                    out=row_vectors[0:1, MODEL_DIM * s : MODEL_DIM * (s + 1)],
                    in_=stream["bias"][2 * MODEL_DIM : OUT_DIM].unsqueeze(0),
                )

            load_tokens(stream_a, 0, 2)
            load_tokens(stream_a, 2, 2)
            load_scales(stream_a)
            load_words(stream_a)
            load_bias_rows(stream_a)
            load_bias_rows(stream_b)
            load_values_bias(stream_a)
            for stream in streams:
                for qk in range(2):
                    column = 2 * MODEL_DIM + P * (2 * stream["index"] + qk)
                    nc.sync.dma_start(out=row_vectors[0:1, column : column + P], in_=stream["gains"][qk].unsqueeze(0))
            load_rope(stream_a, nc.sync)
            load_values_bias(stream_b)
            load_rope(stream_b, nc.sync)
            load_tokens(stream_a, 4, 2)
            for b in range(1, BATCH):
                load_tokens(stream_a, 6 * b, 6)
            for b in range(BATCH):
                load_tokens(stream_b, 2 * b, 2)
            load_words(stream_b)
            load_scales(stream_b)

            nc.vector.tensor_copy(
                out=split_pairs[:].rearrange("p (l m) -> p l m", l=2), in_=ident[:].rearrange("p (m l) -> p l m", l=2)
            )
            for i in range(CHUNK_TILES):
                transpose_tokens(0, i)
            for i in range(CHUNK_TILES):
                regroup_tokens(0, i)
            for i in range(CHUNK_TILES):
                quantise_tokens(0, i)
            bias_ps = psum_y.tile([P, P], F32, tag="y")
            values_bias_a_ps = psum_y.tile([P, MODEL_DIM], F32, tag="y")
            values_bias_b_ps = psum_y.tile([P, MODEL_DIM], F32, tag="y")
            gains_ps = psum_y.tile([P, MODEL_DIM], F32, tag="y")
            nc.scalar.copy(out=bias_rows_f32[:], in_=bias_rows[:])
            nc.tensor.transpose(out=bias_ps[:], in_=bias_rows_f32[:], identity=ident[:])
            nc.scalar.copy(out=bias_columns[:], in_=bias_ps[:, 0 : 2 * QK_SLOTS])
            spread_rows(0, values_bias_a_ps)
            nc.scalar.copy(out=spread[:, 0:MODEL_DIM], in_=values_bias_a_ps[:])

            for tick in range(0, n_heads + LAG_SUM):
                transpose_back(tick - LAG_TRANSPOSE)
                for w, i in transpose_at.get(tick, []):
                    transpose_tokens(w, i)
                multiply(tick)
                for w, k in multiply_at.get(tick, []):
                    multiply_values(w, k)
                if tick == GAINS_TICK:
                    spread_rows(2, gains_ps)
                if tick == GAINS_TICK + 1:
                    spread_rows(1, values_bias_b_ps)
                sum_of_squares(tick - LAG_NORM)
                add_bias(tick - LAG_BIAS)
                inverse_rms(tick - LAG_NORM)
                for w, i in regroup_at.get(tick, []):
                    regroup_tokens(w, i)
                if tick == GAINS_TICK:
                    nc.scalar.copy(out=spread[:, 2 * MODEL_DIM : 3 * MODEL_DIM], in_=gains_ps[:])
                if tick == GAINS_TICK + 1:
                    nc.scalar.copy(out=spread[:, MODEL_DIM : 2 * MODEL_DIM], in_=values_bias_b_ps[:])
                rotation_products(tick - LAG_PRODUCTS)
                for w, k in add_at.get(tick, []):
                    add_values_bias(w, k)
                for w, i in quantise_at.get(tick, []):
                    quantise_tokens(w, i)
                if 0 <= tick - GAINS_TICK < 3:
                    stream, qk = ((stream_a, 0), (stream_b, 0), (stream_b, 1))[tick - GAINS_TICK]
                    for l in range(2):
                        make_table(stream, qk, l, nc.vector, gains_ps)
                if tick == GAINS_TICK:
                    for l in range(2):
                        make_table(stream_a, 1, l, nc.gpsimd, spread[:, 2 * MODEL_DIM : 3 * MODEL_DIM])
                rotation_sum(tick - LAG_SUM)
